import numpy as np
import ml_dtypes


def mxq(x, axis, fmt="e4m3"):
    dtype, down = {"e4m3": (ml_dtypes.float8_e4m3fn, 7), "e5m2": (ml_dtypes.float8_e5m2, 14)}[fmt]
    v = np.moveaxis(np.asarray(x, np.float32).astype(ml_dtypes.bfloat16).astype(np.float64), axis, -1)
    blocks = v.reshape(v.shape[:-1] + (-1, 32))
    amax = np.abs(blocks).max(-1, keepdims=True)
    byte = np.maximum(np.where(amax > 0, np.frexp(amax)[1] - 1 + 127, 0) - down, 1)
    scale = np.exp2(byte - 127.0)
    codes = (blocks / scale).astype(np.float32).astype(dtype).astype(np.float64)
    return np.moveaxis((codes * scale).reshape(v.shape), -1, axis)


WIDE = False


def mx_kscale(k):
    if not WIDE:
        return np.ones(k)
    levels = np.array([10, -10, 5, -5, 0])
    a = np.random.permutation(np.resize(levels, k // 512 * 4)).reshape(k // 512, 4)
    idx = np.arange(k)
    return np.exp2(a[idx // 512, idx % 128 // 32])


BF16 = ml_dtypes.bfloat16


def bf(x):
    return np.asarray(x, np.float32).astype(BF16)


def f64(x):
    return np.asarray(x).astype(np.float64)


D, KW, STRIDE, STACK, B, O = 32, 11, 3, 16, 4096, 128
W_IN = D * D
POS = (D - KW) // STRIDE + 1
K = STACK * POS * POS


def build_mask():
    base_new = np.tile(np.arange(KW), KW)
    addition_new = np.repeat(np.arange(KW) * D, KW)
    index_1 = addition_new + base_new
    index_width = np.tile(index_1, POS)
    addition_width = np.repeat(STRIDE * np.arange(POS), KW * KW)
    index_row = index_width + addition_width
    index_column = np.tile(index_row, POS)
    addition_height = np.repeat(STRIDE * D * np.arange(POS), KW * KW * POS)
    index_final = index_column + addition_height
    stack = np.repeat(np.arange(POS * POS), KW * KW)
    block = np.zeros((POS * POS, W_IN))
    block[stack, index_final] = 1.0
    return np.vstack([block] * STACK)


def setup_inputs():
    s, t = mx_kscale(W_IN), mx_kscale(K)
    return {"z": bf(np.random.standard_normal((B, W_IN)) * s),
            "T3": bf(np.random.standard_normal((K, W_IN)) * 0.7 / np.sqrt(KW * KW) / s),
            "mask": bf(build_mask()),
            "x1": bf(np.random.standard_normal((B, K)) * 0.7 * t),
            "x2": bf(np.random.standard_normal((B, K)) * 1.4 * t),
            "C_w": bf(np.random.standard_normal((O, K)) / np.sqrt(K) / t),
            "C_b": bf(np.random.standard_normal(O) * 0.5)}


def reference(z, T3, mask, x1, x2, C_w, C_b):
    zq = mxq(f64(z).reshape(-1, D * D), 1, "e4m3")
    p3 = zq @ mxq(f64(mask) * f64(T3), 1, "e4m3").T
    x3 = 2.0 * p3 * f64(x2) - f64(x1)
    return (mxq(x3, 1, "e4m3") @ mxq(f64(C_w), 1, "e4m3").T) + f64(C_b)

@@ -1,0 +1,258 @@
+from contextlib import ExitStack
+
+import concourse.mybir as mybir
+from concourse.masks import make_identity
+
+F32 = mybir.dt.float32
+BF16 = mybir.dt.bfloat16
+U32 = mybir.dt.uint32
+U8 = mybir.dt.uint8
+FP8X4 = mybir.dt.float8_e4m3fn_x4
+ALU = mybir.AluOpType
+
+P = 128
+B, KIN, F, O = 4096, 1024, 1024, 128
+NCH = 8
+NJ = 4
+NU = NCH * NJ
+FLOPS = 2 * B * KIN * F + 2 * B * F * O
+
+COMBOS = [(0, 0), (1, 0), (1, 1), (2, 0), (2, 1), (3, 1)]
+Z_BANK_ORDER = [0, 2, 1, 3]
+GPSIMD_EVERY = 2
+PIN = True
+
+
+def tile_chebyshev_l3_sparsed32_stack_pb_t_kernel(tc, z, T3, mask, x1, x2, C_w, C_b, out):
+    nc = tc.nc
+    with ExitStack() as ctx:
+        const = ctx.enter_context(tc.tile_pool(name="const", bufs=1))
+        stream = ctx.enter_context(tc.tile_pool(name="stream", bufs=4))
+        chunkp = ctx.enter_context(tc.tile_pool(name="chunkp", bufs=2))
+        unitp = ctx.enter_context(tc.tile_pool(name="unitp", bufs=4))
+        psum = ctx.enter_context(tc.psum_pool(name="psum", bufs=1))
+        if PIN:
+            ctx.enter_context(tc.manual_schedule())
+
+        zv = z.rearrange("(c p j) k -> c p (j k)", p=P, j=NJ)
+        x1v = x1.rearrange("(c p j) k -> c p (j k)", p=P, j=NJ)
+        x2v = x2.rearrange("(c p j) k -> c p (j k)", p=P, j=NJ)
+        outv = out.rearrange("(c p j) o -> c p (j o)", p=P, j=NJ)
+        t3v = T3.rearrange("(ft q) k -> q ft k", q=P)
+        mkv = mask.rearrange("(ft q) k -> q ft k", q=P)
+
+        ident_f = const.tile([P, P], F32, name="ident_f")
+        make_identity(nc, ident_f[:])
+        ident_b = const.tile([P, P], BF16, name="ident_b")
+        make_identity(nc, ident_b[:])
+
+        t3h = []
+        mkh = []
+        for hh in range(2):
+            t3_t = stream.tile([P, 4 * KIN], BF16, name="t3_%d" % hh, tag="x1")
+            mk_t = stream.tile([P, 4 * KIN], BF16, name="mk_%d" % hh, tag="x2")
+            t3h.append(t3_t)
+            mkh.append(mk_t)
+        for fp in range(4):
+            hh, lo = fp // 2, (fp % 2) * 2 * KIN
+            nc.sync.dma_start(
+                out=t3h[hh][:, lo:lo + 2 * KIN].rearrange("p (f k) -> p f k", f=2),
+                in_=t3v[:, 2 * fp:2 * fp + 2, :])
+            nc.sync.dma_start(
+                out=mkh[hh][:, lo:lo + 2 * KIN].rearrange("p (f k) -> p f k", f=2),
+                in_=mkv[:, 2 * fp:2 * fp + 2, :])
+        c_sb = const.tile([P, F], BF16, name="c_sb")
+        nc.scalar.dma_start(out=c_sb[:], in_=C_w)
+        bias_sb = const.tile([P, O], BF16, name="bias_sb")
+        nc.scalar.dma_start(out=bias_sb[:], in_=C_b.partition_broadcast(P))
+
+        z_sb = {}
+        x1_sb = {}
+        x2_sb = {}
+
+        def load(c):
+            z_sb[c] = stream.tile([P, NJ * KIN], BF16, name="z_%d" % c, tag="z")
+            nc.sync.dma_start(out=z_sb[c][:], in_=zv[c])
+            x2_sb[c] = stream.tile([P, NJ * F], BF16, name="x2_%d" % c, tag="x2")
+            nc.sync.dma_start(out=x2_sb[c][:], in_=x2v[c])
+            x1_sb[c] = stream.tile([P, NJ * F], BF16, name="x1_%d" % c, tag="x1")
+            nc.sync.dma_start(out=x1_sb[c][:], in_=x1v[c])
+
+        load(0)
+        load(1)
+        load(2)
+
+        wg = const.tile([P, 6 * 256 * 4], BF16, name="wg", align_bytes=64)
+        wc = const.tile([P, 6 * 256], U32, name="wc", align_bytes=64)
+        ws = const.tile([P, 6 * 256], U8, name="ws", align_bytes=64)
+        wgw = wg[:].bitcast(F32).rearrange("p (ci s r u) -> p ci s r u", ci=6, s=16, r=16, u=2)
+        for fp in range(4):
+            hh, lo = fp // 2, (fp % 2) * 2 * KIN
+            nc.vector.tensor_tensor(
+                out=t3h[hh][:, lo:lo + 2 * KIN], in0=t3h[hh][:, lo:lo + 2 * KIN],
+                in1=mkh[hh][:, lo:lo + 2 * KIN], op=ALU.mult)
+            ww = t3h[hh][:].bitcast(F32)
+            for g in range(2):
+                wt = psum.tile([P, 2, 256], F32, name="wt", tag="tp", bufs=2)
+                for u in range(2):
+                    for fl in range(2):
+                        col = lo // 2 + fl * 512 + 256 * g + 128 * u
+                        nc.tensor.transpose(wt[:, u, fl * P:(fl + 1) * P], ww[:, col:col + P], ident_f[:])
+                wtv = wt[:].rearrange("p u (s pr r) -> p pr s r u", s=4, pr=4, r=16)
+                for ci in range(6):
+                    pr, gg = COMBOS[ci]
+                    if gg != g:
+                        continue
+                    if g == 0:
+                        nc.scalar.copy(out=wgw[:, ci, 4 * fp:4 * fp + 4, :, :], in_=wtv[:, pr])
+                    else:
+                        nc.vector.tensor_copy(out=wgw[:, ci, 4 * fp:4 * fp + 4, :, :], in_=wtv[:, pr])
+        for i in range(3):
+            nc.vector.quantize_mx(
+                out=wc[:, 512 * i:512 * (i + 1)].bitcast(FP8X4),
+                scales=ws[:, 512 * i:512 * (i + 1)],
+                in_=wg[:, 2048 * i:2048 * (i + 1)])
+
+        cg = const.tile([P, 2 * O * 4], BF16, name="cg", align_bytes=64)
+        cc = const.tile([P, 2 * O], U32, name="cc", align_bytes=64)
+        cs = const.tile([P, 2 * O], U8, name="cs", align_bytes=64)
+        ct = psum.tile([P, 8, P], BF16, name="ct", tag="xt", bufs=2)
+        for gt in range(8):
+            nc.tensor.transpose(ct[:, gt, :], c_sb[:, gt * P:(gt + 1) * P], ident_b[:])
+        nc.scalar.copy(
+            out=cg[:].rearrange("p (g o t) -> p g o t", g=2, t=4),
+            in_=ct[:].rearrange("p (g t) o -> p g o t", g=2))
+        nc.vector.quantize_mx(out=cc[:].bitcast(FP8X4), scales=cs[:], in_=cg[:])
+
+        zg = {}
+        zc = {}
+        zs = {}
+
+        def z_alloc(c):
+            zg[c] = chunkp.tile([P, 2 * 512 * 4], BF16, name="zg_%d" % c, tag="zg", align_bytes=64)
+            zc[c] = chunkp.tile([P, 2 * 512], U32, name="zc_%d" % c, tag="zc", align_bytes=64)
+            zs[c] = chunkp.tile([P, 2 * 512], U8, name="zs_%d" % c, tag="zs", align_bytes=64)
+
+        def z_bank(c, i):
+            g, jh = i // 2, i % 2
+            zw = z_sb[c][:].bitcast(F32)
+            zt = psum.tile([P, 2, 256], F32, name="zt", tag="tp", bufs=2)
+            for u in range(2):
+                for jl in range(2):
+                    col = (2 * jh + jl) * 512 + 256 * g + 128 * u
+                    nc.tensor.transpose(zt[:, u, jl * P:(jl + 1) * P], zw[:, col:col + P], ident_f[:])
+            zgw = zg[c][:].bitcast(F32).rearrange("p (g c u) -> p g c u", g=2, u=2)
+            nc.scalar.copy(out=zgw[:, g, jh * 256:(jh + 1) * 256, :], in_=zt[:].rearrange("p u c -> p c u"))
+
+        def z_quant(c, i):
+            lo = i * 256
+            nc.vector.quantize_mx(
+                out=zc[c][:, lo:lo + 256].bitcast(FP8X4), scales=zs[c][:, lo:lo + 256],
+                in_=zg[c][:, 4 * lo:4 * lo + 1024])
+
+        p3 = {}
+        y_sb = {}
+        x3_sb = {}
+        xg = {}
+        xc = {}
+        xs = {}
+        po = {}
+
+        def mm1(n):
+            c, j = divmod(n, NJ)
+            banks = []
+            for half in range(2):
+                bank = psum.tile([P, 512], F32, name="p3_%d_%d" % (n, half), tag="p3", bufs=3)
+                banks.append(bank)
+            p3[n] = banks
+            for ci in range(6):
+                pr, g = COMBOS[ci]
+                first = ci == 0 or COMBOS[ci - 1][0] != pr
+                last = ci == 5 or COMBOS[ci + 1][0] != pr
+                lo = g * 512 + j * P
+                nc.tensor.matmul_mx(
+                    out=banks[pr // 2][:, (pr % 2) * 256:(pr % 2) * 256 + 256],
+                    lhsT=zc[c][:, lo:lo + P].bitcast(FP8X4), lhsT_scale=zs[c][:, lo:lo + P],
+                    rhs=wc[:, ci * 256:(ci + 1) * 256].bitcast(FP8X4), rhs_scale=ws[:, ci * 256:(ci + 1) * 256],
+                    start=first, stop=last)
+
+        def op1(n):
+            c, j = divmod(n, NJ)
+            y_sb[n] = unitp.tile([P, F], F32, name="y_%d" % n, tag="y")
+            yv = y_sb[n][:].rearrange("p (s q) -> p s q", q=64)
+            x2u = x2_sb[c][:, j * F:(j + 1) * F].rearrange("p (s q) -> p s q", q=64)
+            for pr in range(4):
+                nc.vector.scalar_tensor_tensor(
+                    out=yv[:, :, pr * 16:(pr + 1) * 16],
+                    in0=p3[n][pr // 2][:, (pr % 2) * 256:(pr % 2) * 256 + 256].rearrange("p (s r) -> p s r", r=16),
+                    scalar=2.0,
+                    in1=x2u[:, :, pr * 16:(pr + 1) * 16],
+                    op0=ALU.mult, op1=ALU.mult)
+
+        def op2(n):
+            c, j = divmod(n, NJ)
+            x3_sb[n] = unitp.tile([P, F], BF16, name="x3_%d" % n, tag="x3")
+            eng = nc.gpsimd if (GPSIMD_EVERY and n % GPSIMD_EVERY == GPSIMD_EVERY - 1) else nc.vector
+            eng.tensor_tensor(out=x3_sb[n][:], in0=y_sb[n][:], in1=x1_sb[c][:, j * F:(j + 1) * F], op=ALU.subtract)
+
+        def x_t(n):
+            xt = psum.tile([P, 8, P], BF16, name="xt", tag="xt", bufs=2)
+            for gt in range(8):
+                nc.tensor.transpose(xt[:, gt, :], x3_sb[n][:, gt * P:(gt + 1) * P], ident_b[:])
+            xg[n] = unitp.tile([P, 2 * P * 4], BF16, name="xg_%d" % n, tag="xg", align_bytes=64)
+            nc.scalar.copy(
+                out=xg[n][:].rearrange("p (g b t) -> p g b t", g=2, t=4),
+                in_=xt[:].rearrange("p (g t) b -> p g b t", g=2))
+
+        def x_quant(n):
+            xc[n] = unitp.tile([P, 2 * P], U32, name="xc_%d" % n, tag="xc", align_bytes=64)
+            xs[n] = unitp.tile([P, 2 * P], U8, name="xs_%d" % n, tag="xs", align_bytes=64)
+            nc.vector.quantize_mx(out=xc[n][:].bitcast(FP8X4), scales=xs[n][:], in_=xg[n][:])
+
+        def mm2(n):
+            c, j = divmod(n, NJ)
+            if j == 0:
+                po[c] = psum.tile([P, NJ, O], F32, name="po_%d" % c, tag="po", bufs=1)
+            for g in range(2):
+                nc.tensor.matmul_mx(
+                    out=po[c][:, j, :],
+                    lhsT=xc[n][:, g * P:(g + 1) * P].bitcast(FP8X4), lhsT_scale=xs[n][:, g * P:(g + 1) * P],
+                    rhs=cc[:, g * O:(g + 1) * O].bitcast(FP8X4), rhs_scale=cs[:, g * O:(g + 1) * O],
+                    start=(g == 0), stop=(g == 1))
+
+        def fin(c):
+            o_sb = chunkp.tile([P, NJ, O], F32, name="o_sb", tag="o_sb")
+            nc.vector.tensor_tensor(
+                out=o_sb[:], in0=po[c][:], in1=bias_sb[:].unsqueeze(1).to_broadcast([P, NJ, O]), op=ALU.add)
+            nc.sync.dma_start(out=outv[c], in_=o_sb[:].rearrange("p j o -> p (j o)"))
+
+        z_alloc(0)
+        for i in Z_BANK_ORDER:
+            z_bank(0, i)
+        for i in Z_BANK_ORDER:
+            z_quant(0, i)
+
+        for n in range(NU + 6):
+            c, j = divmod(n, NJ)
+            live = n < NU
+            if live and j == 0 and c + 3 < NCH:
+                load(c + 3)
+            if live and c + 1 < NCH:
+                if j == 0:
+                    z_alloc(c + 1)
+                z_bank(c + 1, Z_BANK_ORDER[j])
+            if 0 <= n - 3 < NU:
+                x_t(n - 3)
+            if live:
+                mm1(n)
+            if 0 <= n - 5 < NU:
+                mm2(n - 5)
+            if live:
+                op1(n)
+                op2(n)
+            if 1 <= n <= NU and (n - 1) // NJ + 1 < NCH:
+                z_quant((n - 1) // NJ + 1, Z_BANK_ORDER[(n - 1) % NJ])
+            if 0 <= n - 4 < NU:
+                x_quant(n - 4)
+            if 0 <= n - 5 < NU and (n - 5) % NJ == NJ - 1:
+                fin((n - 5) // NJ)

@@ -19,7 +19,7 @@ FLOPS = 2 * B * KIN * F + 2 * B * F * O
 
 COMBOS = [(0, 0), (1, 0), (1, 1), (2, 0), (2, 1), (3, 1)]
 Z_BANK_ORDER = [0, 2, 1, 3]
-GPSIMD_EVERY = 2
+GPS = True
 PIN = True
 
 
@@ -93,7 +93,7 @@ def tile_chebyshev_l3_sparsed32_stack_pb_t_kernel(tc, z, T3, mask, x1, x2, C_w, 
                 in1=mkh[hh][:, lo:lo + 2 * KIN], op=ALU.mult)
             ww = t3h[hh][:].bitcast(F32)
             for g in range(2):
-                wt = psum.tile([P, 2, 256], F32, name="wt", tag="tp", bufs=2)
+                wt = psum.tile([P, 2, 256], F32, name="wt", tag="p3", bufs=5)
                 for u in range(2):
                     for fl in range(2):
                         col = lo // 2 + fl * 512 + 256 * g + 128 * u
@@ -116,7 +116,7 @@ def tile_chebyshev_l3_sparsed32_stack_pb_t_kernel(tc, z, T3, mask, x1, x2, C_w, 
         cg = const.tile([P, 2 * O * 4], BF16, name="cg", align_bytes=64)
         cc = const.tile([P, 2 * O], U32, name="cc", align_bytes=64)
         cs = const.tile([P, 2 * O], U8, name="cs", align_bytes=64)
-        ct = psum.tile([P, 8, P], BF16, name="ct", tag="xt", bufs=2)
+        ct = psum.tile([P, 8, P], BF16, name="ct", tag="xt", bufs=1)
         for gt in range(8):
             nc.tensor.transpose(ct[:, gt, :], c_sb[:, gt * P:(gt + 1) * P], ident_b[:])
         nc.scalar.copy(
@@ -133,10 +133,10 @@ def tile_chebyshev_l3_sparsed32_stack_pb_t_kernel(tc, z, T3, mask, x1, x2, C_w, 
             zc[c] = chunkp.tile([P, 2 * 512], U32, name="zc_%d" % c, tag="zc", align_bytes=64)
             zs[c] = chunkp.tile([P, 2 * 512], U8, name="zs_%d" % c, tag="zs", align_bytes=64)
 
-        def z_bank(c, i):
+        def z_bank(c, i, early=False):
             g, jh = i // 2, i % 2
             zw = z_sb[c][:].bitcast(F32)
-            zt = psum.tile([P, 2, 256], F32, name="zt", tag="tp", bufs=2)
+            zt = psum.tile([P, 2, 256], F32, name="zt", tag=("p3" if early else "tp"), bufs=(5 if early else 1))
             for u in range(2):
                 for jl in range(2):
                     col = (2 * jh + jl) * 512 + 256 * g + 128 * u
@@ -162,7 +162,7 @@ def tile_chebyshev_l3_sparsed32_stack_pb_t_kernel(tc, z, T3, mask, x1, x2, C_w, 
             c, j = divmod(n, NJ)
             banks = []
             for half in range(2):
-                bank = psum.tile([P, 512], F32, name="p3_%d_%d" % (n, half), tag="p3", bufs=3)
+                bank = psum.tile([P, 512], F32, name="p3_%d_%d" % (n, half), tag="p3", bufs=5)
                 banks.append(bank)
             p3[n] = banks
             for ci in range(6):
@@ -189,14 +189,13 @@ def tile_chebyshev_l3_sparsed32_stack_pb_t_kernel(tc, z, T3, mask, x1, x2, C_w, 
                     in1=x2u[:, :, pr * 16:(pr + 1) * 16],
                     op0=ALU.mult, op1=ALU.mult)
 
-        def op2(n):
+        def op2(n, eng):
             c, j = divmod(n, NJ)
             x3_sb[n] = unitp.tile([P, F], BF16, name="x3_%d" % n, tag="x3")
-            eng = nc.gpsimd if (GPSIMD_EVERY and n % GPSIMD_EVERY == GPSIMD_EVERY - 1) else nc.vector
             eng.tensor_tensor(out=x3_sb[n][:], in0=y_sb[n][:], in1=x1_sb[c][:, j * F:(j + 1) * F], op=ALU.subtract)
 
         def x_t(n):
-            xt = psum.tile([P, 8, P], BF16, name="xt", tag="xt", bufs=2)
+            xt = psum.tile([P, 8, P], BF16, name="xt", tag="xt", bufs=1)
             for gt in range(8):
                 nc.tensor.transpose(xt[:, gt, :], x3_sb[n][:, gt * P:(gt + 1) * P], ident_b[:])
             xg[n] = unitp.tile([P, 2 * P * 4], BF16, name="xg_%d" % n, tag="xg", align_bytes=64)
@@ -205,8 +204,8 @@ def tile_chebyshev_l3_sparsed32_stack_pb_t_kernel(tc, z, T3, mask, x1, x2, C_w, 
                 in_=xt[:].rearrange("p (g t) b -> p g b t", g=2))
 
         def x_quant(n):
-            xc[n] = unitp.tile([P, 2 * P], U32, name="xc_%d" % n, tag="xc", align_bytes=64)
-            xs[n] = unitp.tile([P, 2 * P], U8, name="xs_%d" % n, tag="xs", align_bytes=64)
+            xc[n] = unitp.tile([P, 2 * P], U32, name="xc_%d" % n, tag="xc", bufs=6, align_bytes=64)
+            xs[n] = unitp.tile([P, 2 * P], U8, name="xs_%d" % n, tag="xs", bufs=6, align_bytes=64)
             nc.vector.quantize_mx(out=xc[n][:].bitcast(FP8X4), scales=xs[n][:], in_=xg[n][:])
 
         def mm2(n):
@@ -226,33 +225,60 @@ def tile_chebyshev_l3_sparsed32_stack_pb_t_kernel(tc, z, T3, mask, x1, x2, C_w, 
                 out=o_sb[:], in0=po[c][:], in1=bias_sb[:].unsqueeze(1).to_broadcast([P, NJ, O]), op=ALU.add)
             nc.sync.dma_start(out=outv[c], in_=o_sb[:].rearrange("p j o -> p (j o)"))
 
-        z_alloc(0)
-        for i in Z_BANK_ORDER:
-            z_bank(0, i)
-        for i in Z_BANK_ORDER:
-            z_quant(0, i)
 
-        for n in range(NU + 6):
-            c, j = divmod(n, NJ)
-            live = n < NU
-            if live and j == 0 and c + 3 < NCH:
-                load(c + 3)
-            if live and c + 1 < NCH:
-                if j == 0:
-                    z_alloc(c + 1)
-                z_bank(c + 1, Z_BANK_ORDER[j])
-            if 0 <= n - 3 < NU:
-                x_t(n - 3)
-            if live:
-                mm1(n)
-            if 0 <= n - 5 < NU:
-                mm2(n - 5)
-            if live:
-                op1(n)
-                op2(n)
-            if 1 <= n <= NU and (n - 1) // NJ + 1 < NCH:
-                z_quant((n - 1) // NJ + 1, Z_BANK_ORDER[(n - 1) % NJ])
-            if 0 <= n - 4 < NU:
-                x_quant(n - 4)
-            if 0 <= n - 5 < NU and (n - 5) % NJ == NJ - 1:
-                fin((n - 5) // NJ)
+        mark = const.tile([P, 1], BF16, name="mark")
+
+        def z_bank_m(m, early=False):
+            if m < 4 * NCH:
+                if m % 4 == 0:
+                    z_alloc(m // 4)
+                z_bank(m // 4, Z_BANK_ORDER[m % 4], early)
+
+        def z_quant_m(m):
+            if 4 <= m < 4 * NCH:
+                z_quant(m // 4, Z_BANK_ORDER[m % 4])
+
+        def ok(n):
+            return 0 <= n < NU
+
+        for m in range(4):
+            z_bank_m(m, True)
+        for m in range(4):
+            z_quant(0, Z_BANK_ORDER[m])
+
+        for k in range(-1, NU // 2 + 4):
+            a_now, b_now = 2 * k, 2 * k + 1
+            if GPS and ok(a_now - 2):
+                nc.gpsimd.tensor_copy(out=mark[:], in_=x3_sb[b_now - 2][:, 0:1])
+                op2(a_now - 2, nc.gpsimd)
+            if k >= 0 and k % 2 == 0 and k // 2 + 3 < NCH:
+                load(k // 2 + 3)
+            if ok(a_now + 2):
+                mm1(a_now + 2)
+            if ok(a_now - 6):
+                mm2(a_now - 6)
+            z_bank_m(2 * k + 6)
+            if ok(b_now - 2):
+                x_t(b_now - 2)
+            if ok(b_now + 2):
+                mm1(b_now + 2)
+            if ok(b_now - 6):
+                mm2(b_now - 6)
+            z_bank_m(2 * k + 7)
+            if ok(a_now - 2):
+                x_t(a_now - 2)
+            if k >= 5 and k % 2 == 1:
+                fin((k - 5) // 2)
+            if ok(a_now):
+                op1(a_now)
+                op1(b_now)
+            z_quant_m(2 * k + 5)
+            if ok(a_now - 4):
+                x_quant(a_now - 4)
+            z_quant_m(2 * k + 6)
+            if ok(b_now - 2):
+                x_quant(b_now - 2)
+            if ok(a_now):
+                if not GPS:
+                    op2(a_now, nc.vector)
+                op2(b_now, nc.vector)

@@ -19,7 +19,7 @@ FLOPS = 2 * B * KIN * F + 2 * B * F * O
 
 COMBOS = [(0, 0), (1, 0), (1, 1), (2, 0), (2, 1), (3, 1)]
 Z_BANK_ORDER = [0, 2, 1, 3]
-GPS = True
+GPS = False
 PIN = True
 
 

@@ -19,7 +19,6 @@ FLOPS = 2 * B * KIN * F + 2 * B * F * O
 
 COMBOS = [(0, 0), (1, 0), (1, 1), (2, 0), (2, 1), (3, 1)]
 Z_BANK_ORDER = [0, 2, 1, 3]
-GPS = False
 PIN = True
 
 
@@ -46,6 +45,24 @@ def tile_chebyshev_l3_sparsed32_stack_pb_t_kernel(tc, z, T3, mask, x1, x2, C_w, 
         ident_b = const.tile([P, P], BF16, name="ident_b")
         make_identity(nc, ident_b[:])
 
+        z_sb = {}
+        x1_sb = {}
+        x2_sb = {}
+        HALF = NJ * KIN // 2
+
+        def load_half(dst, src, c, hf, tag):
+            t = stream.tile([P, HALF], BF16, name="%s_%d_%d" % (tag, c, hf), tag=tag)
+            nc.sync.dma_start(out=t[:], in_=src[c][:, hf * HALF:(hf + 1) * HALF])
+            for jl in range(2):
+                dst[NJ * c + 2 * hf + jl] = t[:, jl * KIN:(jl + 1) * KIN]
+
+        def load_whole(dst, src, c, tag):
+            t = stream.tile([P, NJ * KIN], BF16, name="%s_%d" % (tag, c), tag=tag)
+            nc.sync.dma_start(out=t[:], in_=src[c])
+            for j in range(NJ):
+                dst[NJ * c + j] = t[:, j * KIN:(j + 1) * KIN]
+
+        load_half(z_sb, zv, 0, 0, "z")
         t3h = []
         mkh = []
         for hh in range(2):
@@ -66,19 +83,16 @@ def tile_chebyshev_l3_sparsed32_stack_pb_t_kernel(tc, z, T3, mask, x1, x2, C_w, 
         bias_sb = const.tile([P, O], BF16, name="bias_sb")
         nc.scalar.dma_start(out=bias_sb[:], in_=C_b.partition_broadcast(P))
 
-        z_sb = {}
-        x1_sb = {}
-        x2_sb = {}
-
         def load(c):
-            z_sb[c] = stream.tile([P, NJ * KIN], BF16, name="z_%d" % c, tag="z")
-            nc.sync.dma_start(out=z_sb[c][:], in_=zv[c])
-            x2_sb[c] = stream.tile([P, NJ * F], BF16, name="x2_%d" % c, tag="x2")
-            nc.sync.dma_start(out=x2_sb[c][:], in_=x2v[c])
-            x1_sb[c] = stream.tile([P, NJ * F], BF16, name="x1_%d" % c, tag="x1")
-            nc.sync.dma_start(out=x1_sb[c][:], in_=x1v[c])
+            load_whole(z_sb, zv, c, "z")
+            load_whole(x2_sb, x2v, c, "x2")
+            load_whole(x1_sb, x1v, c, "x1")
 
-        load(0)
+        load_half(x2_sb, x2v, 0, 0, "x2")
+        load_half(z_sb, zv, 0, 1, "z")
+        load_half(x1_sb, x1v, 0, 0, "x1")
+        load_half(x2_sb, x2v, 0, 1, "x2")
+        load_half(x1_sb, x1v, 0, 1, "x1")
         load(1)
         load(2)
 
@@ -107,11 +121,11 @@ def tile_chebyshev_l3_sparsed32_stack_pb_t_kernel(tc, z, T3, mask, x1, x2, C_w, 
                         nc.scalar.copy(out=wgw[:, ci, 4 * fp:4 * fp + 4, :, :], in_=wtv[:, pr])
                     else:
                         nc.vector.tensor_copy(out=wgw[:, ci, 4 * fp:4 * fp + 4, :, :], in_=wtv[:, pr])
-        for i in range(3):
-            nc.vector.quantize_mx(
-                out=wc[:, 512 * i:512 * (i + 1)].bitcast(FP8X4),
-                scales=ws[:, 512 * i:512 * (i + 1)],
-                in_=wg[:, 2048 * i:2048 * (i + 1)])
+            for ci in range(6):
+                lo_w = ci * 256 + 64 * fp
+                nc.vector.quantize_mx(
+                    out=wc[:, lo_w:lo_w + 64].bitcast(FP8X4), scales=ws[:, lo_w:lo_w + 64],
+                    in_=wg[:, 4 * lo_w:4 * lo_w + 256])
 
         cg = const.tile([P, 2 * O * 4], BF16, name="cg", align_bytes=64)
         cc = const.tile([P, 2 * O], U32, name="cc", align_bytes=64)
@@ -135,11 +149,11 @@ def tile_chebyshev_l3_sparsed32_stack_pb_t_kernel(tc, z, T3, mask, x1, x2, C_w, 
 
         def z_bank(c, i, early=False):
             g, jh = i // 2, i % 2
-            zw = z_sb[c][:].bitcast(F32)
             zt = psum.tile([P, 2, 256], F32, name="zt", tag=("p3" if early else "tp"), bufs=(5 if early else 1))
             for u in range(2):
                 for jl in range(2):
-                    col = (2 * jh + jl) * 512 + 256 * g + 128 * u
+                    col = 256 * g + 128 * u
+                    zw = z_sb[NJ * c + 2 * jh + jl].bitcast(F32)
                     nc.tensor.transpose(zt[:, u, jl * P:(jl + 1) * P], zw[:, col:col + P], ident_f[:])
             zgw = zg[c][:].bitcast(F32).rearrange("p (g c u) -> p g c u", g=2, u=2)
             nc.scalar.copy(out=zgw[:, g, jh * 256:(jh + 1) * 256, :], in_=zt[:].rearrange("p u c -> p c u"))
@@ -158,14 +172,14 @@ def tile_chebyshev_l3_sparsed32_stack_pb_t_kernel(tc, z, T3, mask, x1, x2, C_w, 
         xs = {}
         po = {}
 
-        def mm1(n):
+        def mm1(n, half):
             c, j = divmod(n, NJ)
-            banks = []
-            for half in range(2):
-                bank = psum.tile([P, 512], F32, name="p3_%d_%d" % (n, half), tag="p3", bufs=5)
-                banks.append(bank)
-            p3[n] = banks
-            for ci in range(6):
+            bank = psum.tile([P, 512], F32, name="p3_%d_%d" % (n, half), tag="p3", bufs=5)
+            if half == 0:
+                p3[n] = []
+            p3[n].append(bank)
+            banks = p3[n]
+            for ci in range(3 * half, 3 * half + 3):
                 pr, g = COMBOS[ci]
                 first = ci == 0 or COMBOS[ci - 1][0] != pr
                 last = ci == 5 or COMBOS[ci + 1][0] != pr
@@ -180,7 +194,7 @@ def tile_chebyshev_l3_sparsed32_stack_pb_t_kernel(tc, z, T3, mask, x1, x2, C_w, 
             c, j = divmod(n, NJ)
             y_sb[n] = unitp.tile([P, F], F32, name="y_%d" % n, tag="y")
             yv = y_sb[n][:].rearrange("p (s q) -> p s q", q=64)
-            x2u = x2_sb[c][:, j * F:(j + 1) * F].rearrange("p (s q) -> p s q", q=64)
+            x2u = x2_sb[n].rearrange("p (s q) -> p s q", q=64)
             for pr in range(4):
                 nc.vector.scalar_tensor_tensor(
                     out=yv[:, :, pr * 16:(pr + 1) * 16],
@@ -192,16 +206,21 @@ def tile_chebyshev_l3_sparsed32_stack_pb_t_kernel(tc, z, T3, mask, x1, x2, C_w, 
         def op2(n, eng):
             c, j = divmod(n, NJ)
             x3_sb[n] = unitp.tile([P, F], BF16, name="x3_%d" % n, tag="x3")
-            eng.tensor_tensor(out=x3_sb[n][:], in0=y_sb[n][:], in1=x1_sb[c][:, j * F:(j + 1) * F], op=ALU.subtract)
+            eng.tensor_tensor(out=x3_sb[n][:], in0=y_sb[n][:], in1=x1_sb[n], op=ALU.subtract)
 
-        def x_t(n):
-            xt = psum.tile([P, 8, P], BF16, name="xt", tag="xt", bufs=1)
+        def x_t(n, tail=False, on_vector=False):
+            xt = psum.tile([P, 8, P], BF16, name="xt", tag=("p3" if tail else "xt"), bufs=(5 if tail else 1))
             for gt in range(8):
                 nc.tensor.transpose(xt[:, gt, :], x3_sb[n][:, gt * P:(gt + 1) * P], ident_b[:])
-            xg[n] = unitp.tile([P, 2 * P * 4], BF16, name="xg_%d" % n, tag="xg", align_bytes=64)
-            nc.scalar.copy(
-                out=xg[n][:].rearrange("p (g b t) -> p g b t", g=2, t=4),
-                in_=xt[:].rearrange("p (g t) b -> p g b t", g=2))
+            xg[n] = unitp.tile([P, 2 * P * 4], BF16, name="xg_%d" % n, tag="xg", bufs=6, align_bytes=64)
+            if on_vector:
+                nc.vector.tensor_copy(
+                    out=xg[n][:].rearrange("p (g b t) -> p g b t", g=2, t=4),
+                    in_=xt[:].rearrange("p (g t) b -> p g b t", g=2))
+            else:
+                nc.scalar.copy(
+                    out=xg[n][:].rearrange("p (g b t) -> p g b t", g=2, t=4),
+                    in_=xt[:].rearrange("p (g t) b -> p g b t", g=2))
 
         def x_quant(n):
             xc[n] = unitp.tile([P, 2 * P], U32, name="xc_%d" % n, tag="xc", bufs=6, align_bytes=64)
@@ -246,39 +265,57 @@ def tile_chebyshev_l3_sparsed32_stack_pb_t_kernel(tc, z, T3, mask, x1, x2, C_w, 
         for m in range(4):
             z_quant(0, Z_BANK_ORDER[m])
 
-        for k in range(-1, NU // 2 + 4):
+        for k in range(-1, NU // 2):
             a_now, b_now = 2 * k, 2 * k + 1
-            if GPS and ok(a_now - 2):
+            if ok(a_now - 2):
                 nc.gpsimd.tensor_copy(out=mark[:], in_=x3_sb[b_now - 2][:, 0:1])
                 op2(a_now - 2, nc.gpsimd)
             if k >= 0 and k % 2 == 0 and k // 2 + 3 < NCH:
                 load(k // 2 + 3)
+            if k >= 6 and k % 2 == 0:
+                fin((k - 6) // 2)
             if ok(a_now + 2):
-                mm1(a_now + 2)
-            if ok(a_now - 6):
-                mm2(a_now - 6)
+                mm1(a_now + 2, 0)
             z_bank_m(2 * k + 6)
+            if ok(a_now - 4):
+                x_t(a_now - 4)
+            if ok(a_now + 2):
+                mm1(a_now + 2, 1)
+                mm1(b_now + 2, 0)
+            if ok(a_now - 8):
+                mm2(a_now - 8)
+                mm2(b_now - 8)
+            z_bank_m(2 * k + 7)
             if ok(b_now - 2):
                 x_t(b_now - 2)
             if ok(b_now + 2):
-                mm1(b_now + 2)
-            if ok(b_now - 6):
-                mm2(b_now - 6)
-            z_bank_m(2 * k + 7)
-            if ok(a_now - 2):
-                x_t(a_now - 2)
-            if k >= 5 and k % 2 == 1:
-                fin((k - 5) // 2)
+                mm1(b_now + 2, 1)
             if ok(a_now):
                 op1(a_now)
                 op1(b_now)
+            z_quant_m(2 * k + 4)
+            if ok(a_now - 6):
+                x_quant(a_now - 6)
             z_quant_m(2 * k + 5)
-            if ok(a_now - 4):
-                x_quant(a_now - 4)
-            z_quant_m(2 * k + 6)
-            if ok(b_now - 2):
-                x_quant(b_now - 2)
+            if ok(b_now - 4):
+                x_quant(b_now - 4)
             if ok(a_now):
-                if not GPS:
+                if k == NU // 2 - 1:
                     op2(a_now, nc.vector)
                 op2(b_now, nc.vector)
+
+        fin(NCH - 3)
+        x_t(NU - 4, True, False)
+        x_t(NU - 2, True, True)
+        x_t(NU - 1, True, False)
+        x_quant(NU - 6)
+        x_quant(NU - 3)
+        for n in range(NU - 8, NU - 4):
+            mm2(n)
+        fin(NCH - 2)
+        x_quant(NU - 4)
+        x_quant(NU - 2)
+        x_quant(NU - 1)
+        for n in range(NU - 4, NU):
+            mm2(n)
+        fin(NCH - 1)

@@ -13,13 +13,11 @@ ALU = mybir.AluOpType
 P = 128
 B, KIN, F, O = 4096, 1024, 1024, 128
 NCH = 8
-NJ = 4
-NU = NCH * NJ
+NPAIR = 16
 FLOPS = 2 * B * KIN * F + 2 * B * F * O
 
-COMBOS = [(0, 0), (1, 0), (1, 1), (2, 0), (2, 1), (3, 1)]
-Z_BANK_ORDER = [0, 2, 1, 3]
-PIN = True
+G_OF_PR = [[0], [0, 1], [0, 1], [1]]
+CI = {(0, 0): 0, (1, 0): 1, (1, 1): 2, (2, 0): 3, (2, 1): 4, (3, 1): 5}
 
 
 def tile_chebyshev_l3_sparsed32_stack_pb_t_kernel(tc, z, T3, mask, x1, x2, C_w, C_b, out):
@@ -27,16 +25,13 @@ def tile_chebyshev_l3_sparsed32_stack_pb_t_kernel(tc, z, T3, mask, x1, x2, C_w, 
     with ExitStack() as ctx:
         const = ctx.enter_context(tc.tile_pool(name="const", bufs=1))
         stream = ctx.enter_context(tc.tile_pool(name="stream", bufs=4))
-        chunkp = ctx.enter_context(tc.tile_pool(name="chunkp", bufs=2))
-        unitp = ctx.enter_context(tc.tile_pool(name="unitp", bufs=4))
+        work = ctx.enter_context(tc.tile_pool(name="work", bufs=3))
         psum = ctx.enter_context(tc.psum_pool(name="psum", bufs=1))
-        if PIN:
-            ctx.enter_context(tc.manual_schedule())
 
-        zv = z.rearrange("(c p j) k -> c p (j k)", p=P, j=NJ)
-        x1v = x1.rearrange("(c p j) k -> c p (j k)", p=P, j=NJ)
-        x2v = x2.rearrange("(c p j) k -> c p (j k)", p=P, j=NJ)
-        outv = out.rearrange("(c p j) o -> c p (j o)", p=P, j=NJ)
+        zv = z.rearrange("(c p j) k -> c p (j k)", p=P, j=4)
+        x1v = x1.rearrange("(c p j) k -> c p (j k)", p=P, j=4)
+        x2v = x2.rearrange("(c p j) k -> c p (j k)", p=P, j=4)
+        outv = out.rearrange("(c p j) o -> c p (j o)", p=P, j=4)
         t3v = T3.rearrange("(ft q) k -> q ft k", q=P)
         mkv = mask.rearrange("(ft q) k -> q ft k", q=P)
 
@@ -48,19 +43,18 @@ def tile_chebyshev_l3_sparsed32_stack_pb_t_kernel(tc, z, T3, mask, x1, x2, C_w, 
         z_sb = {}
         x1_sb = {}
         x2_sb = {}
-        HALF = NJ * KIN // 2
+        PW = 2 * KIN
 
         def load_half(dst, src, c, hf, tag):
-            t = stream.tile([P, HALF], BF16, name="%s_%d_%d" % (tag, c, hf), tag=tag)
-            nc.sync.dma_start(out=t[:], in_=src[c][:, hf * HALF:(hf + 1) * HALF])
-            for jl in range(2):
-                dst[NJ * c + 2 * hf + jl] = t[:, jl * KIN:(jl + 1) * KIN]
+            t = stream.tile([P, PW], BF16, name="%s_%d_%d" % (tag, c, hf), tag=tag)
+            nc.sync.dma_start(out=t[:], in_=src[c][:, hf * PW:(hf + 1) * PW])
+            dst[2 * c + hf] = t[:]
 
         def load_whole(dst, src, c, tag):
-            t = stream.tile([P, NJ * KIN], BF16, name="%s_%d" % (tag, c), tag=tag)
+            t = stream.tile([P, 2 * PW], BF16, name="%s_%d" % (tag, c), tag=tag)
             nc.sync.dma_start(out=t[:], in_=src[c])
-            for j in range(NJ):
-                dst[NJ * c + j] = t[:, j * KIN:(j + 1) * KIN]
+            for hf in range(2):
+                dst[2 * c + hf] = t[:, hf * PW:(hf + 1) * PW]
 
         load_half(z_sb, zv, 0, 0, "z")
         t3h = []
@@ -82,25 +76,48 @@ def tile_chebyshev_l3_sparsed32_stack_pb_t_kernel(tc, z, T3, mask, x1, x2, C_w, 
         nc.scalar.dma_start(out=c_sb[:], in_=C_w)
         bias_sb = const.tile([P, O], BF16, name="bias_sb")
         nc.scalar.dma_start(out=bias_sb[:], in_=C_b.partition_broadcast(P))
-
-        def load(c):
-            load_whole(z_sb, zv, c, "z")
-            load_whole(x2_sb, x2v, c, "x2")
-            load_whole(x1_sb, x1v, c, "x1")
-
         load_half(x2_sb, x2v, 0, 0, "x2")
         load_half(z_sb, zv, 0, 1, "z")
+        load_half(z_sb, zv, 1, 0, "z")
         load_half(x1_sb, x1v, 0, 0, "x1")
         load_half(x2_sb, x2v, 0, 1, "x2")
         load_half(x1_sb, x1v, 0, 1, "x1")
-        load(1)
-        load(2)
+        load_half(z_sb, zv, 1, 1, "z")
+        load_half(x2_sb, x2v, 1, 0, "x2")
+        load_half(x1_sb, x1v, 1, 0, "x1")
+        load_whole(z_sb, zv, 2, "z")
+        load_half(x2_sb, x2v, 1, 1, "x2")
+        load_half(x1_sb, x1v, 1, 1, "x1")
+        load_whole(z_sb, zv, 3, "z")
+        later_loads = {1: (2, 4), 2: (3, 5), 3: (4, 6), 4: (5, None), 5: (None, 7), 6: (6, None), 8: (7, None)}
+
+        zg = {}
+        zc = {}
+        zs = {}
+
+        def z_t(k, g, early=False):
+            if g == 0:
+                zg[k] = work.tile([P, 2 * 256 * 4], BF16, name="zg_%d" % k, tag="zg", align_bytes=64)
+            zw = z_sb[k].bitcast(F32)
+            zt = psum.tile([P, 2, 256], F32, name="zt", tag=("p3" if early else "tp"), bufs=(5 if early else 1))
+            for u in range(2):
+                for jl in range(2):
+                    col = jl * 512 + 256 * g + 128 * u
+                    nc.tensor.transpose(zt[:, u, jl * P:(jl + 1) * P], zw[:, col:col + P], ident_f[:])
+            zgw = zg[k][:].bitcast(F32).rearrange("p (g c u) -> p g c u", g=2, u=2)
+            nc.scalar.copy(out=zgw[:, g, :, :], in_=zt[:].rearrange("p u c -> p c u"))
+
+        def z_q(k):
+            zc[k] = work.tile([P, 512], U32, name="zc_%d" % k, tag="zc", bufs=4, align_bytes=64)
+            zs[k] = work.tile([P, 512], U8, name="zs_%d" % k, tag="zs", bufs=4, align_bytes=64)
+            nc.vector.quantize_mx(out=zc[k][:].bitcast(FP8X4), scales=zs[k][:], in_=zg[k][:])
 
         wg = const.tile([P, 6 * 256 * 4], BF16, name="wg", align_bytes=64)
         wc = const.tile([P, 6 * 256], U32, name="wc", align_bytes=64)
         ws = const.tile([P, 6 * 256], U8, name="ws", align_bytes=64)
         wgw = wg[:].bitcast(F32).rearrange("p (ci s r u) -> p ci s r u", ci=6, s=16, r=16, u=2)
-        for fp in range(4):
+
+        def w_prep(fp):
             hh, lo = fp // 2, (fp % 2) * 2 * KIN
             nc.vector.tensor_tensor(
                 out=t3h[hh][:, lo:lo + 2 * KIN], in0=t3h[hh][:, lo:lo + 2 * KIN],
@@ -113,14 +130,13 @@ def tile_chebyshev_l3_sparsed32_stack_pb_t_kernel(tc, z, T3, mask, x1, x2, C_w, 
                         col = lo // 2 + fl * 512 + 256 * g + 128 * u
                         nc.tensor.transpose(wt[:, u, fl * P:(fl + 1) * P], ww[:, col:col + P], ident_f[:])
                 wtv = wt[:].rearrange("p u (s pr r) -> p pr s r u", s=4, pr=4, r=16)
-                for ci in range(6):
-                    pr, gg = COMBOS[ci]
-                    if gg != g:
-                        continue
-                    if g == 0:
-                        nc.scalar.copy(out=wgw[:, ci, 4 * fp:4 * fp + 4, :, :], in_=wtv[:, pr])
-                    else:
-                        nc.vector.tensor_copy(out=wgw[:, ci, 4 * fp:4 * fp + 4, :, :], in_=wtv[:, pr])
+                for pr in range(4):
+                    if g in G_OF_PR[pr]:
+                        dst = wgw[:, CI[(pr, g)], 4 * fp:4 * fp + 4, :, :]
+                        if g == 0:
+                            nc.scalar.copy(out=dst, in_=wtv[:, pr])
+                        else:
+                            nc.vector.tensor_copy(out=dst, in_=wtv[:, pr])
             for ci in range(6):
                 lo_w = ci * 256 + 64 * fp
                 nc.vector.quantize_mx(
@@ -130,39 +146,17 @@ def tile_chebyshev_l3_sparsed32_stack_pb_t_kernel(tc, z, T3, mask, x1, x2, C_w, 
         cg = const.tile([P, 2 * O * 4], BF16, name="cg", align_bytes=64)
         cc = const.tile([P, 2 * O], U32, name="cc", align_bytes=64)
         cs = const.tile([P, 2 * O], U8, name="cs", align_bytes=64)
-        ct = psum.tile([P, 8, P], BF16, name="ct", tag="xt", bufs=1)
-        for gt in range(8):
-            nc.tensor.transpose(ct[:, gt, :], c_sb[:, gt * P:(gt + 1) * P], ident_b[:])
-        nc.scalar.copy(
-            out=cg[:].rearrange("p (g o t) -> p g o t", g=2, t=4),
-            in_=ct[:].rearrange("p (g t) o -> p g o t", g=2))
-        nc.vector.quantize_mx(out=cc[:].bitcast(FP8X4), scales=cs[:], in_=cg[:])
 
-        zg = {}
-        zc = {}
-        zs = {}
+        def c_t():
+            ct = psum.tile([P, 8, P], BF16, name="ct", tag="xt", bufs=1)
+            for gt in range(8):
+                nc.tensor.transpose(ct[:, gt, :], c_sb[:, gt * P:(gt + 1) * P], ident_b[:])
+            nc.scalar.copy(
+                out=cg[:].rearrange("p (g o t) -> p g o t", g=2, t=4),
+                in_=ct[:].rearrange("p (g t) o -> p g o t", g=2))
 
-        def z_alloc(c):
-            zg[c] = chunkp.tile([P, 2 * 512 * 4], BF16, name="zg_%d" % c, tag="zg", align_bytes=64)
-            zc[c] = chunkp.tile([P, 2 * 512], U32, name="zc_%d" % c, tag="zc", align_bytes=64)
-            zs[c] = chunkp.tile([P, 2 * 512], U8, name="zs_%d" % c, tag="zs", align_bytes=64)
-
-        def z_bank(c, i, early=False):
-            g, jh = i // 2, i % 2
-            zt = psum.tile([P, 2, 256], F32, name="zt", tag=("p3" if early else "tp"), bufs=(5 if early else 1))
-            for u in range(2):
-                for jl in range(2):
-                    col = 256 * g + 128 * u
-                    zw = z_sb[NJ * c + 2 * jh + jl].bitcast(F32)
-                    nc.tensor.transpose(zt[:, u, jl * P:(jl + 1) * P], zw[:, col:col + P], ident_f[:])
-            zgw = zg[c][:].bitcast(F32).rearrange("p (g c u) -> p g c u", g=2, u=2)
-            nc.scalar.copy(out=zgw[:, g, jh * 256:(jh + 1) * 256, :], in_=zt[:].rearrange("p u c -> p c u"))
-
-        def z_quant(c, i):
-            lo = i * 256
-            nc.vector.quantize_mx(
-                out=zc[c][:, lo:lo + 256].bitcast(FP8X4), scales=zs[c][:, lo:lo + 256],
-                in_=zg[c][:, 4 * lo:4 * lo + 1024])
+        def c_q():
+            nc.vector.quantize_mx(out=cc[:].bitcast(FP8X4), scales=cs[:], in_=cg[:])
 
         p3 = {}
         y_sb = {}
@@ -172,150 +166,152 @@ def tile_chebyshev_l3_sparsed32_stack_pb_t_kernel(tc, z, T3, mask, x1, x2, C_w, 
         xs = {}
         po = {}
 
-        def mm1(n, half):
-            c, j = divmod(n, NJ)
-            bank = psum.tile([P, 512], F32, name="p3_%d_%d" % (n, half), tag="p3", bufs=5)
-            if half == 0:
-                p3[n] = []
-            p3[n].append(bank)
-            banks = p3[n]
-            for ci in range(3 * half, 3 * half + 3):
-                pr, g = COMBOS[ci]
-                first = ci == 0 or COMBOS[ci - 1][0] != pr
-                last = ci == 5 or COMBOS[ci + 1][0] != pr
-                lo = g * 512 + j * P
-                nc.tensor.matmul_mx(
-                    out=banks[pr // 2][:, (pr % 2) * 256:(pr % 2) * 256 + 256],
-                    lhsT=zc[c][:, lo:lo + P].bitcast(FP8X4), lhsT_scale=zs[c][:, lo:lo + P],
-                    rhs=wc[:, ci * 256:(ci + 1) * 256].bitcast(FP8X4), rhs_scale=ws[:, ci * 256:(ci + 1) * 256],
-                    start=first, stop=last)
+        def mm1(k, pr):
+            bank = psum.tile([P, 512], F32, name="p3_%d_%d" % (k, pr), tag="p3", bufs=5)
+            p3[(k, pr)] = bank
+            gs = G_OF_PR[pr]
+            for jl in range(2):
+                for g in gs:
+                    lo = g * 256 + jl * P
+                    ci = CI[(pr, g)]
+                    nc.tensor.matmul_mx(
+                        out=bank[:, jl * 256:(jl + 1) * 256],
+                        lhsT=zc[k][:, lo:lo + P].bitcast(FP8X4), lhsT_scale=zs[k][:, lo:lo + P],
+                        rhs=wc[:, ci * 256:(ci + 1) * 256].bitcast(FP8X4), rhs_scale=ws[:, ci * 256:(ci + 1) * 256],
+                        start=(g == gs[0]), stop=(g == gs[-1]))
 
-        def op1(n):
-            c, j = divmod(n, NJ)
-            y_sb[n] = unitp.tile([P, F], F32, name="y_%d" % n, tag="y")
-            yv = y_sb[n][:].rearrange("p (s q) -> p s q", q=64)
-            x2u = x2_sb[n].rearrange("p (s q) -> p s q", q=64)
+        def op1(k):
+            y_sb[k] = work.tile([P, PW], F32, name="y_%d" % k, tag="y")
+            yv = y_sb[k][:].rearrange("p (s q) -> p s q", q=64)
+            x2u = x2_sb[k].rearrange("p (s q) -> p s q", q=64)
             for pr in range(4):
                 nc.vector.scalar_tensor_tensor(
                     out=yv[:, :, pr * 16:(pr + 1) * 16],
-                    in0=p3[n][pr // 2][:, (pr % 2) * 256:(pr % 2) * 256 + 256].rearrange("p (s r) -> p s r", r=16),
+                    in0=p3[(k, pr)][:].rearrange("p (s r) -> p s r", r=16),
                     scalar=2.0,
                     in1=x2u[:, :, pr * 16:(pr + 1) * 16],
                     op0=ALU.mult, op1=ALU.mult)
 
-        def op2(n, eng):
-            c, j = divmod(n, NJ)
-            x3_sb[n] = unitp.tile([P, F], BF16, name="x3_%d" % n, tag="x3")
-            eng.tensor_tensor(out=x3_sb[n][:], in0=y_sb[n][:], in1=x1_sb[n], op=ALU.subtract)
+        def op2(k, unit, eng):
+            if k not in x3_sb:
+                x3_sb[k] = work.tile([P, PW], BF16, name="x3_%d" % k, tag="x3", bufs=4)
+            cols = slice(unit * F, (unit + 1) * F)
+            eng.tensor_tensor(out=x3_sb[k][:, cols], in0=y_sb[k][:, cols], in1=x1_sb[k][:, cols], op=ALU.subtract)
 
-        def x_t(n, tail=False, on_vector=False):
+        def x_t(k, unit, tail=False, on_vector=False):
             xt = psum.tile([P, 8, P], BF16, name="xt", tag=("p3" if tail else "xt"), bufs=(5 if tail else 1))
             for gt in range(8):
-                nc.tensor.transpose(xt[:, gt, :], x3_sb[n][:, gt * P:(gt + 1) * P], ident_b[:])
-            xg[n] = unitp.tile([P, 2 * P * 4], BF16, name="xg_%d" % n, tag="xg", bufs=6, align_bytes=64)
+                col = unit * F + gt * P
+                nc.tensor.transpose(xt[:, gt, :], x3_sb[k][:, col:col + P], ident_b[:])
+            if unit == 0:
+                xg[k] = work.tile([P, 2 * 1024], BF16, name="xg_%d" % k, tag="xg", align_bytes=64)
+            dst = xg[k][:, unit * 1024:(unit + 1) * 1024].rearrange("p (g b t) -> p g b t", g=2, t=4)
+            src = xt[:].rearrange("p (g t) b -> p g b t", g=2)
             if on_vector:
-                nc.vector.tensor_copy(
-                    out=xg[n][:].rearrange("p (g b t) -> p g b t", g=2, t=4),
-                    in_=xt[:].rearrange("p (g t) b -> p g b t", g=2))
+                nc.vector.tensor_copy(out=dst, in_=src)
             else:
-                nc.scalar.copy(
-                    out=xg[n][:].rearrange("p (g b t) -> p g b t", g=2, t=4),
-                    in_=xt[:].rearrange("p (g t) b -> p g b t", g=2))
+                nc.scalar.copy(out=dst, in_=src)
 
-        def x_quant(n):
-            xc[n] = unitp.tile([P, 2 * P], U32, name="xc_%d" % n, tag="xc", bufs=6, align_bytes=64)
-            xs[n] = unitp.tile([P, 2 * P], U8, name="xs_%d" % n, tag="xs", bufs=6, align_bytes=64)
-            nc.vector.quantize_mx(out=xc[n][:].bitcast(FP8X4), scales=xs[n][:], in_=xg[n][:])
+        def x_q(k):
+            xc[k] = work.tile([P, 512], U32, name="xc_%d" % k, tag="xc", align_bytes=64)
+            xs[k] = work.tile([P, 512], U8, name="xs_%d" % k, tag="xs", align_bytes=64)
+            nc.vector.quantize_mx(out=xc[k][:].bitcast(FP8X4), scales=xs[k][:], in_=xg[k][:])
 
-        def mm2(n):
-            c, j = divmod(n, NJ)
-            if j == 0:
-                po[c] = psum.tile([P, NJ, O], F32, name="po_%d" % c, tag="po", bufs=1)
-            for g in range(2):
-                nc.tensor.matmul_mx(
-                    out=po[c][:, j, :],
-                    lhsT=xc[n][:, g * P:(g + 1) * P].bitcast(FP8X4), lhsT_scale=xs[n][:, g * P:(g + 1) * P],
-                    rhs=cc[:, g * O:(g + 1) * O].bitcast(FP8X4), rhs_scale=cs[:, g * O:(g + 1) * O],
-                    start=(g == 0), stop=(g == 1))
+        def mm2(k):
+            c = k // 2
+            if k % 2 == 0:
+                po[c] = psum.tile([P, 4, O], F32, name="po_%d" % c, tag="po", bufs=1)
+            for unit in range(2):
+                for g in range(2):
+                    lo = (unit * 2 + g) * P
+                    nc.tensor.matmul_mx(
+                        out=po[c][:, (k % 2) * 2 + unit, :],
+                        lhsT=xc[k][:, lo:lo + P].bitcast(FP8X4), lhsT_scale=xs[k][:, lo:lo + P],
+                        rhs=cc[:, g * O:(g + 1) * O].bitcast(FP8X4), rhs_scale=cs[:, g * O:(g + 1) * O],
+                        start=(g == 0), stop=(g == 1))
 
         def fin(c):
-            o_sb = chunkp.tile([P, NJ, O], F32, name="o_sb", tag="o_sb")
+            o_sb = work.tile([P, 4, O], F32, name="o_sb", tag="o_sb", bufs=2)
             nc.vector.tensor_tensor(
-                out=o_sb[:], in0=po[c][:], in1=bias_sb[:].unsqueeze(1).to_broadcast([P, NJ, O]), op=ALU.add)
+                out=o_sb[:], in0=po[c][:], in1=bias_sb[:].unsqueeze(1).to_broadcast([P, 4, O]), op=ALU.add)
             nc.sync.dma_start(out=outv[c], in_=o_sb[:].rearrange("p j o -> p (j o)"))
 
-
         mark = const.tile([P, 1], BF16, name="mark")
+        z_t(0, 0, True)
+        z_t(0, 1, True)
+        z_q(0)
+        for fp in range(4):
+            w_prep(fp)
+        z_t(1, 0, True)
+        z_t(1, 1, True)
+        z_q(1)
 
-        def z_bank_m(m, early=False):
-            if m < 4 * NCH:
-                if m % 4 == 0:
-                    z_alloc(m // 4)
-                z_bank(m // 4, Z_BANK_ORDER[m % 4], early)
-
-        def z_quant_m(m):
-            if 4 <= m < 4 * NCH:
-                z_quant(m // 4, Z_BANK_ORDER[m % 4])
-
-        def ok(n):
-            return 0 <= n < NU
-
-        for m in range(4):
-            z_bank_m(m, True)
-        for m in range(4):
-            z_quant(0, Z_BANK_ORDER[m])
-
-        for k in range(-1, NU // 2):
-            a_now, b_now = 2 * k, 2 * k + 1
-            if ok(a_now - 2):
-                nc.gpsimd.tensor_copy(out=mark[:], in_=x3_sb[b_now - 2][:, 0:1])
-                op2(a_now - 2, nc.gpsimd)
-            if k >= 0 and k % 2 == 0 and k // 2 + 3 < NCH:
-                load(k // 2 + 3)
+        for k in range(-1, NPAIR):
+            if k >= 1:
+                nc.gpsimd.tensor_copy(out=mark[:], in_=x3_sb[k - 1][:, F:F + 1])
+                op2(k - 1, 0, nc.gpsimd)
+            if k in later_loads:
+                cx, cz = later_loads[k]
+                if cx is not None:
+                    load_whole(x2_sb, x2v, cx, "x2")
+                    load_whole(x1_sb, x1v, cx, "x1")
+                if cz is not None:
+                    load_whole(z_sb, zv, cz, "z")
             if k >= 6 and k % 2 == 0:
                 fin((k - 6) // 2)
-            if ok(a_now + 2):
-                mm1(a_now + 2, 0)
-            z_bank_m(2 * k + 6)
-            if ok(a_now - 4):
-                x_t(a_now - 4)
-            if ok(a_now + 2):
-                mm1(a_now + 2, 1)
-                mm1(b_now + 2, 0)
-            if ok(a_now - 8):
-                mm2(a_now - 8)
-                mm2(b_now - 8)
-            z_bank_m(2 * k + 7)
-            if ok(b_now - 2):
-                x_t(b_now - 2)
-            if ok(b_now + 2):
-                mm1(b_now + 2, 1)
-            if ok(a_now):
-                op1(a_now)
-                op1(b_now)
-            z_quant_m(2 * k + 4)
-            if ok(a_now - 6):
-                x_quant(a_now - 6)
-            z_quant_m(2 * k + 5)
-            if ok(b_now - 4):
-                x_quant(b_now - 4)
-            if ok(a_now):
-                if k == NU // 2 - 1:
-                    op2(a_now, nc.vector)
-                op2(b_now, nc.vector)
+            if k == 0:
+                zts = [(2, 0), (2, 1)]
+            elif k == 1:
+                zts = [(3, 0), (3, 1), (4, 0), (4, 1)]
+            elif 2 <= k and k + 3 < NPAIR:
+                zts = [(k + 3, 0), (k + 3, 1)]
+            else:
+                zts = []
+            half = len(zts) // 2
+            nxt = k + 1 < NPAIR
+            if nxt:
+                mm1(k + 1, 0)
+            for kz, g in zts[:half]:
+                z_t(kz, g)
+            if k >= 2:
+                x_t(k - 2, 0)
+            if nxt:
+                mm1(k + 1, 1)
+                mm1(k + 1, 2)
+            if k >= 4:
+                mm2(k - 4)
+            for kz, g in zts[half:]:
+                z_t(kz, g)
+            if k == 0:
+                c_t()
+            if k >= 2:
+                x_t(k - 2, 1)
+            if nxt:
+                mm1(k + 1, 3)
+            if k >= 0:
+                op1(k)
+            if k == 0:
+                c_q()
+            if k >= 3:
+                x_q(k - 3)
+            if 0 <= k and k + 2 < NPAIR:
+                z_q(k + 2)
+            if k >= 0:
+                if k == NPAIR - 1:
+                    op2(k, 0, nc.vector)
+                op2(k, 1, nc.vector)
 
         fin(NCH - 3)
-        x_t(NU - 4, True, False)
-        x_t(NU - 2, True, True)
-        x_t(NU - 1, True, False)
-        x_quant(NU - 6)
-        x_quant(NU - 3)
-        for n in range(NU - 8, NU - 4):
-            mm2(n)
+        x_t(NPAIR - 2, 0, True, False)
+        x_t(NPAIR - 2, 1, True, True)
+        x_q(NPAIR - 3)
+        x_t(NPAIR - 1, 0, True, False)
+        x_t(NPAIR - 1, 1, True, True)
+        mm2(NPAIR - 4)
+        mm2(NPAIR - 3)
+        x_q(NPAIR - 2)
         fin(NCH - 2)
-        x_quant(NU - 4)
-        x_quant(NU - 2)
-        x_quant(NU - 1)
-        for n in range(NU - 4, NU):
-            mm2(n)
+        x_q(NPAIR - 1)
+        mm2(NPAIR - 2)
+        mm2(NPAIR - 1)
         fin(NCH - 1)

@@ -17,7 +17,7 @@ NPAIR = 16
 FLOPS = 2 * B * KIN * F + 2 * B * F * O
 
 G_OF_PR = [[0], [0, 1], [0, 1], [1]]
-CI = {(0, 0): 0, (1, 0): 1, (1, 1): 2, (2, 0): 3, (2, 1): 4, (3, 1): 5}
+CI = {(0, 0): 0, (1, 0): 1, (2, 0): 2, (1, 1): 5, (2, 1): 6, (3, 1): 7}
 
 
 def tile_chebyshev_l3_sparsed32_stack_pb_t_kernel(tc, z, T3, mask, x1, x2, C_w, C_b, out):
@@ -27,6 +27,7 @@ def tile_chebyshev_l3_sparsed32_stack_pb_t_kernel(tc, z, T3, mask, x1, x2, C_w, 
         stream = ctx.enter_context(tc.tile_pool(name="stream", bufs=4))
         work = ctx.enter_context(tc.tile_pool(name="work", bufs=3))
         psum = ctx.enter_context(tc.psum_pool(name="psum", bufs=1))
+        ctx.enter_context(tc.manual_schedule())
 
         zv = z.rearrange("(c p j) k -> c p (j k)", p=P, j=4)
         x1v = x1.rearrange("(c p j) k -> c p (j k)", p=P, j=4)
@@ -112,16 +113,23 @@ def tile_chebyshev_l3_sparsed32_stack_pb_t_kernel(tc, z, T3, mask, x1, x2, C_w, 
             zs[k] = work.tile([P, 512], U8, name="zs_%d" % k, tag="zs", bufs=4, align_bytes=64)
             nc.vector.quantize_mx(out=zc[k][:].bitcast(FP8X4), scales=zs[k][:], in_=zg[k][:])
 
-        wg = const.tile([P, 6 * 256 * 4], BF16, name="wg", align_bytes=64)
-        wc = const.tile([P, 6 * 256], U32, name="wc", align_bytes=64)
-        ws = const.tile([P, 6 * 256], U8, name="ws", align_bytes=64)
-        wgw = wg[:].bitcast(F32).rearrange("p (ci s r u) -> p ci s r u", ci=6, s=16, r=16, u=2)
+        wg = const.tile([P, 8 * 256 * 4], BF16, name="wg", align_bytes=64)
+        wc = const.tile([P, 8 * 256], U32, name="wc", align_bytes=64)
+        ws = const.tile([P, 8 * 256], U8, name="ws", align_bytes=64)
+        wgw = wg[:].bitcast(F32).rearrange("p (g pr s r u) -> p g s pr r u", g=2, pr=4, s=16, r=16, u=2)
 
-        def w_prep(fp):
+        def w_mul(fp, parts):
             hh, lo = fp // 2, (fp % 2) * 2 * KIN
-            nc.vector.tensor_tensor(
-                out=t3h[hh][:, lo:lo + 2 * KIN], in0=t3h[hh][:, lo:lo + 2 * KIN],
-                in1=mkh[hh][:, lo:lo + 2 * KIN], op=ALU.mult)
+            tv = t3h[hh][:, lo:lo + 2 * KIN].rearrange("p (f k) -> p f k", f=2)
+            mv = mkh[hh][:, lo:lo + 2 * KIN].rearrange("p (f k) -> p f k", f=2)
+            w = KIN // parts
+            for i in range(parts):
+                nc.vector.tensor_tensor(
+                    out=tv[:, :, i * w:(i + 1) * w], in0=tv[:, :, i * w:(i + 1) * w],
+                    in1=mv[:, :, i * w:(i + 1) * w], op=ALU.mult)
+
+        def w_t(fp, second_on_vector):
+            hh, lo = fp // 2, (fp % 2) * 2 * KIN
             ww = t3h[hh][:].bitcast(F32)
             for g in range(2):
                 wt = psum.tile([P, 2, 256], F32, name="wt", tag="p3", bufs=5)
@@ -129,19 +137,20 @@ def tile_chebyshev_l3_sparsed32_stack_pb_t_kernel(tc, z, T3, mask, x1, x2, C_w, 
                     for fl in range(2):
                         col = lo // 2 + fl * 512 + 256 * g + 128 * u
                         nc.tensor.transpose(wt[:, u, fl * P:(fl + 1) * P], ww[:, col:col + P], ident_f[:])
-                wtv = wt[:].rearrange("p u (s pr r) -> p pr s r u", s=4, pr=4, r=16)
-                for pr in range(4):
-                    if g in G_OF_PR[pr]:
-                        dst = wgw[:, CI[(pr, g)], 4 * fp:4 * fp + 4, :, :]
-                        if g == 0:
-                            nc.scalar.copy(out=dst, in_=wtv[:, pr])
-                        else:
-                            nc.vector.tensor_copy(out=dst, in_=wtv[:, pr])
-            for ci in range(6):
-                lo_w = ci * 256 + 64 * fp
-                nc.vector.quantize_mx(
-                    out=wc[:, lo_w:lo_w + 64].bitcast(FP8X4), scales=ws[:, lo_w:lo_w + 64],
-                    in_=wg[:, 4 * lo_w:4 * lo_w + 256])
+                src = wt[:].rearrange("p u (s pr r) -> p s pr r u", s=4, pr=4, r=16)
+                dst = wgw[:, g, 4 * fp:4 * fp + 4, :, :, :]
+                if g == 1 and second_on_vector:
+                    nc.vector.tensor_copy(out=dst, in_=src)
+                else:
+                    nc.scalar.copy(out=dst, in_=src)
+
+        def w_q(fp):
+            for pr in range(4):
+                for g in G_OF_PR[pr]:
+                    lo_w = CI[(pr, g)] * 256 + 64 * fp
+                    nc.vector.quantize_mx(
+                        out=wc[:, lo_w:lo_w + 64].bitcast(FP8X4), scales=ws[:, lo_w:lo_w + 64],
+                        in_=wg[:, 4 * lo_w:4 * lo_w + 256])
 
         cg = const.tile([P, 2 * O * 4], BF16, name="cg", align_bytes=64)
         cc = const.tile([P, 2 * O], U32, name="cc", align_bytes=64)
@@ -198,30 +207,40 @@ def tile_chebyshev_l3_sparsed32_stack_pb_t_kernel(tc, z, T3, mask, x1, x2, C_w, 
             cols = slice(unit * F, (unit + 1) * F)
             eng.tensor_tensor(out=x3_sb[k][:, cols], in0=y_sb[k][:, cols], in1=x1_sb[k][:, cols], op=ALU.subtract)
 
-        def x_t(k, unit, tail=False, on_vector=False):
-            xt = psum.tile([P, 8, P], BF16, name="xt", tag=("p3" if tail else "xt"), bufs=(5 if tail else 1))
-            for gt in range(8):
-                col = unit * F + gt * P
-                nc.tensor.transpose(xt[:, gt, :], x3_sb[k][:, col:col + P], ident_b[:])
+        def x_t(k, unit, tail=False, split=False):
             if unit == 0:
-                xg[k] = work.tile([P, 2 * 1024], BF16, name="xg_%d" % k, tag="xg", align_bytes=64)
+                xg[k] = work.tile([P, 2 * 1024], BF16, name="xg_%d" % k, tag="xg", bufs=4, align_bytes=64)
             dst = xg[k][:, unit * 1024:(unit + 1) * 1024].rearrange("p (g b t) -> p g b t", g=2, t=4)
-            src = xt[:].rearrange("p (g t) b -> p g b t", g=2)
-            if on_vector:
-                nc.vector.tensor_copy(out=dst, in_=src)
+            if split:
+                for g in range(2):
+                    xh = psum.tile([P, 4, P], BF16, name="xh", tag="p3", bufs=5)
+                    for t in range(4):
+                        col = unit * F + (4 * g + t) * P
+                        nc.tensor.transpose(xh[:, t, :], x3_sb[k][:, col:col + P], ident_b[:])
+                    if g == 0:
+                        nc.scalar.copy(out=dst[:, g], in_=xh[:].rearrange("p t b -> p b t"))
+                    else:
+                        nc.vector.tensor_copy(out=dst[:, g], in_=xh[:].rearrange("p t b -> p b t"))
             else:
-                nc.scalar.copy(out=dst, in_=src)
+                xt = psum.tile([P, 8, P], BF16, name="xt", tag=("p3" if tail else "xt"), bufs=(5 if tail else 1))
+                for gt in range(8):
+                    col = unit * F + gt * P
+                    nc.tensor.transpose(xt[:, gt, :], x3_sb[k][:, col:col + P], ident_b[:])
+                nc.scalar.copy(out=dst, in_=xt[:].rearrange("p (g t) b -> p g b t", g=2))
 
-        def x_q(k):
-            xc[k] = work.tile([P, 512], U32, name="xc_%d" % k, tag="xc", align_bytes=64)
-            xs[k] = work.tile([P, 512], U8, name="xs_%d" % k, tag="xs", align_bytes=64)
-            nc.vector.quantize_mx(out=xc[k][:].bitcast(FP8X4), scales=xs[k][:], in_=xg[k][:])
+        def x_q(k, units):
+            if k not in xc:
+                xc[k] = work.tile([P, 512], U32, name="xc_%d" % k, tag="xc", align_bytes=64)
+                xs[k] = work.tile([P, 512], U8, name="xs_%d" % k, tag="xs", align_bytes=64)
+            lo, n = units[0] * 256, len(units) * 256
+            nc.vector.quantize_mx(
+                out=xc[k][:, lo:lo + n].bitcast(FP8X4), scales=xs[k][:, lo:lo + n], in_=xg[k][:, 4 * lo:4 * (lo + n)])
 
-        def mm2(k):
+        def mm2(k, units):
             c = k // 2
-            if k % 2 == 0:
+            if c not in po:
                 po[c] = psum.tile([P, 4, O], F32, name="po_%d" % c, tag="po", bufs=1)
-            for unit in range(2):
+            for unit in units:
                 for g in range(2):
                     lo = (unit * 2 + g) * P
                     nc.tensor.matmul_mx(
@@ -237,16 +256,33 @@ def tile_chebyshev_l3_sparsed32_stack_pb_t_kernel(tc, z, T3, mask, x1, x2, C_w, 
             nc.sync.dma_start(out=outv[c], in_=o_sb[:].rearrange("p j o -> p (j o)"))
 
         mark = const.tile([P, 1], BF16, name="mark")
+        BOTH = [0, 1]
         z_t(0, 0, True)
         z_t(0, 1, True)
         z_q(0)
-        for fp in range(4):
-            w_prep(fp)
-        z_t(1, 0, True)
+        c_t()
+        c_q()
+        w_mul(0, 1)
+        w_t(0, False)
+        w_mul(1, 1)
+        w_t(1, False)
+        w_mul(2, 1)
+        w_q(0)
+        w_t(2, False)
+        w_q(1)
+        w_mul(3, 2)
+        w_q(2)
+        w_t(3, True)
+        w_q(3)
+        z_t(1, 0)
         z_t(1, 1, True)
-        z_q(1)
+        for pr in range(4):
+            mm1(0, pr)
+        z_t(2, 0)
+        z_t(2, 1)
 
-        for k in range(-1, NPAIR):
+        for k in range(NPAIR):
+            last = k == NPAIR - 1
             if k >= 1:
                 nc.gpsimd.tensor_copy(out=mark[:], in_=x3_sb[k - 1][:, F:F + 1])
                 op2(k - 1, 0, nc.gpsimd)
@@ -260,58 +296,51 @@ def tile_chebyshev_l3_sparsed32_stack_pb_t_kernel(tc, z, T3, mask, x1, x2, C_w, 
             if k >= 6 and k % 2 == 0:
                 fin((k - 6) // 2)
             if k == 0:
-                zts = [(2, 0), (2, 1)]
-            elif k == 1:
-                zts = [(3, 0), (3, 1), (4, 0), (4, 1)]
-            elif 2 <= k and k + 3 < NPAIR:
-                zts = [(k + 3, 0), (k + 3, 1)]
-            else:
-                zts = []
-            half = len(zts) // 2
-            nxt = k + 1 < NPAIR
-            if nxt:
+                op1(0)
+                z_q(1)
+            if not last:
                 mm1(k + 1, 0)
-            for kz, g in zts[:half]:
-                z_t(kz, g)
+            if k + 3 < NPAIR:
+                z_t(k + 3, 0)
             if k >= 2:
                 x_t(k - 2, 0)
-            if nxt:
+            if not last:
                 mm1(k + 1, 1)
                 mm1(k + 1, 2)
             if k >= 4:
-                mm2(k - 4)
-            for kz, g in zts[half:]:
-                z_t(kz, g)
-            if k == 0:
-                c_t()
+                mm2(k - 4, BOTH)
+            if k + 3 < NPAIR:
+                z_t(k + 3, 1)
             if k >= 2:
                 x_t(k - 2, 1)
-            if nxt:
+            if not last:
                 mm1(k + 1, 3)
-            if k >= 0:
+            if k >= 1:
                 op1(k)
-            if k == 0:
-                c_q()
-            if k >= 3:
-                x_q(k - 3)
-            if 0 <= k and k + 2 < NPAIR:
-                z_q(k + 2)
-            if k >= 0:
-                if k == NPAIR - 1:
-                    op2(k, 0, nc.vector)
+            if last:
+                op2(k, 0, nc.vector)
+                op2(k, 1, nc.vector)
+            else:
+                if k >= 3:
+                    x_q(k - 3, BOTH)
+                if k + 2 < NPAIR:
+                    z_q(k + 2)
                 op2(k, 1, nc.vector)
 
-        fin(NCH - 3)
-        x_t(NPAIR - 2, 0, True, False)
-        x_t(NPAIR - 2, 1, True, True)
-        x_q(NPAIR - 3)
-        x_t(NPAIR - 1, 0, True, False)
+        x_t(NPAIR - 2, 0, True)
+        x_t(NPAIR - 2, 1, True)
+        x_t(NPAIR - 1, 0, True)
         x_t(NPAIR - 1, 1, True, True)
-        mm2(NPAIR - 4)
-        mm2(NPAIR - 3)
-        x_q(NPAIR - 2)
+        x_q(NPAIR - 4, BOTH)
+        fin(NCH - 3)
+        mm2(NPAIR - 4, BOTH)
+        x_q(NPAIR - 3, BOTH)
+        mm2(NPAIR - 3, BOTH)
+        x_q(NPAIR - 2, BOTH)
         fin(NCH - 2)
-        x_q(NPAIR - 1)
-        mm2(NPAIR - 2)
-        mm2(NPAIR - 1)
+        mm2(NPAIR - 2, BOTH)
+        x_q(NPAIR - 1, [0])
+        mm2(NPAIR - 1, [0])
+        x_q(NPAIR - 1, [1])
+        mm2(NPAIR - 1, [1])
         fin(NCH - 1)

@@ -16,6 +16,8 @@ NCH = 8
 NPAIR = 16
 FLOPS = 2 * B * KIN * F + 2 * B * F * O
 
+GP_SHORT = 704
+GP_LONG = 960
 G_OF_PR = [[0], [0, 1], [0, 1], [1]]
 CI = {(0, 0): 0, (1, 0): 1, (2, 0): 2, (1, 1): 5, (2, 1): 6, (3, 1): 7}
 
@@ -201,10 +203,10 @@ def tile_chebyshev_l3_sparsed32_stack_pb_t_kernel(tc, z, T3, mask, x1, x2, C_w, 
                     in1=x2u[:, :, pr * 16:(pr + 1) * 16],
                     op0=ALU.mult, op1=ALU.mult)
 
-        def op2(k, unit, eng):
+        def op2(k, lo, hi, eng):
             if k not in x3_sb:
                 x3_sb[k] = work.tile([P, PW], BF16, name="x3_%d" % k, tag="x3", bufs=4)
-            cols = slice(unit * F, (unit + 1) * F)
+            cols = slice(lo, hi)
             eng.tensor_tensor(out=x3_sb[k][:, cols], in0=y_sb[k][:, cols], in1=x1_sb[k][:, cols], op=ALU.subtract)
 
         def x_t(k, unit, tail=False, split=False):
@@ -257,6 +259,9 @@ def tile_chebyshev_l3_sparsed32_stack_pb_t_kernel(tc, z, T3, mask, x1, x2, C_w, 
 
         mark = const.tile([P, 1], BF16, name="mark")
         BOTH = [0, 1]
+
+        def gp_cols(k):
+            return GP_LONG if ((k + 1) % 2 == 0 and k + 1 >= 6) else GP_SHORT
         z_t(0, 0, True)
         z_t(0, 1, True)
         z_q(0)
@@ -285,7 +290,7 @@ def tile_chebyshev_l3_sparsed32_stack_pb_t_kernel(tc, z, T3, mask, x1, x2, C_w, 
             last = k == NPAIR - 1
             if k >= 1:
                 nc.gpsimd.tensor_copy(out=mark[:], in_=x3_sb[k - 1][:, F:F + 1])
-                op2(k - 1, 0, nc.gpsimd)
+                op2(k - 1, 0, gp_cols(k - 1), nc.gpsimd)
             if k in later_loads:
                 cx, cz = later_loads[k]
                 if cx is not None:
@@ -318,14 +323,14 @@ def tile_chebyshev_l3_sparsed32_stack_pb_t_kernel(tc, z, T3, mask, x1, x2, C_w, 
             if k >= 1:
                 op1(k)
             if last:
-                op2(k, 0, nc.vector)
-                op2(k, 1, nc.vector)
+                op2(k, 0, F, nc.vector)
+                op2(k, F, PW, nc.vector)
             else:
                 if k >= 3:
                     x_q(k - 3, BOTH)
                 if k + 2 < NPAIR:
                     z_q(k + 2)
-                op2(k, 1, nc.vector)
+                op2(k, gp_cols(k), PW, nc.vector)
 
         x_t(NPAIR - 2, 0, True)
         x_t(NPAIR - 2, 1, True)

@@ -16,6 +16,7 @@ NCH = 8
 NPAIR = 16
 FLOPS = 2 * B * KIN * F + 2 * B * F * O
 
+N_PLAIN = 6
 GP_SHORT = 704
 GP_LONG = 960
 G_OF_PR = [[0], [0, 1], [0, 1], [1]]
@@ -227,7 +228,11 @@ def tile_chebyshev_l3_sparsed32_stack_pb_t_kernel(tc, z, T3, mask, x1, x2, C_w, 
                 xt = psum.tile([P, 8, P], BF16, name="xt", tag=("p3" if tail else "xt"), bufs=(5 if tail else 1))
                 for gt in range(8):
                     col = unit * F + gt * P
-                    nc.tensor.transpose(xt[:, gt, :], x3_sb[k][:, col:col + P], ident_b[:])
+                    if gt < N_PLAIN:
+                        nc.tensor.matmul(
+                            out=xt[:, gt, :], lhsT=x3_sb[k][:, col:col + P], rhs=ident_b[:], start=True, stop=True)
+                    else:
+                        nc.tensor.transpose(xt[:, gt, :], x3_sb[k][:, col:col + P], ident_b[:])
                 nc.scalar.copy(out=dst, in_=xt[:].rearrange("p (g t) b -> p g b t", g=2))
 
         def x_q(k, units):
@@ -305,21 +310,20 @@ def tile_chebyshev_l3_sparsed32_stack_pb_t_kernel(tc, z, T3, mask, x1, x2, C_w, 
                 z_q(1)
             if not last:
                 mm1(k + 1, 0)
-            if k + 3 < NPAIR:
-                z_t(k + 3, 0)
+                mm1(k + 1, 1)
             if k >= 2:
                 x_t(k - 2, 0)
+            if k + 3 < NPAIR:
+                z_t(k + 3, 0)
             if not last:
-                mm1(k + 1, 1)
                 mm1(k + 1, 2)
+                mm1(k + 1, 3)
             if k >= 4:
                 mm2(k - 4, BOTH)
-            if k + 3 < NPAIR:
-                z_t(k + 3, 1)
             if k >= 2:
                 x_t(k - 2, 1)
-            if not last:
-                mm1(k + 1, 3)
+            if k + 3 < NPAIR:
+                z_t(k + 3, 1)
             if k >= 1:
                 op1(k)
             if last:

from contextlib import ExitStack

import concourse.mybir as mybir
from concourse.masks import make_identity

F32 = mybir.dt.float32
BF16 = mybir.dt.bfloat16
U32 = mybir.dt.uint32
U8 = mybir.dt.uint8
FP8X4 = mybir.dt.float8_e4m3fn_x4
ALU = mybir.AluOpType

P = 128
B, KIN, F, O = 4096, 1024, 1024, 128
NCH = 8
NPAIR = 16
FLOPS = 2 * B * KIN * F + 2 * B * F * O

N_PLAIN = 6
GP_SHORT = 704
GP_LONG = 960
G_OF_PR = [[0], [0, 1], [0, 1], [1]]
CI = {(0, 0): 0, (1, 0): 1, (2, 0): 2, (1, 1): 5, (2, 1): 6, (3, 1): 7}


def tile_chebyshev_l3_sparsed32_stack_pb_t_kernel(tc, z, T3, mask, x1, x2, C_w, C_b, out):
    nc = tc.nc
    with ExitStack() as ctx:
        const = ctx.enter_context(tc.tile_pool(name="const", bufs=1))
        stream = ctx.enter_context(tc.tile_pool(name="stream", bufs=4))
        work = ctx.enter_context(tc.tile_pool(name="work", bufs=3))
        psum = ctx.enter_context(tc.psum_pool(name="psum", bufs=1))
        ctx.enter_context(tc.manual_schedule())

        zv = z.rearrange("(c p j) k -> c p (j k)", p=P, j=4)
        x1v = x1.rearrange("(c p j) k -> c p (j k)", p=P, j=4)
        x2v = x2.rearrange("(c p j) k -> c p (j k)", p=P, j=4)
        outv = out.rearrange("(c p j) o -> c p (j o)", p=P, j=4)
        t3v = T3.rearrange("(ft q) k -> q ft k", q=P)
        mkv = mask.rearrange("(ft q) k -> q ft k", q=P)

        ident_f = const.tile([P, P], F32, name="ident_f")
        make_identity(nc, ident_f[:])
        ident_b = const.tile([P, P], BF16, name="ident_b")
        make_identity(nc, ident_b[:])

        z_sb = {}
        x1_sb = {}
        x2_sb = {}
        PW = 2 * KIN

        def load_half(dst, src, c, hf, tag):
            t = stream.tile([P, PW], BF16, name="%s_%d_%d" % (tag, c, hf), tag=tag)
            nc.sync.dma_start(out=t[:], in_=src[c][:, hf * PW:(hf + 1) * PW])
            dst[2 * c + hf] = t[:]

        def load_whole(dst, src, c, tag):
            t = stream.tile([P, 2 * PW], BF16, name="%s_%d" % (tag, c), tag=tag)
            nc.sync.dma_start(out=t[:], in_=src[c])
            for hf in range(2):
                dst[2 * c + hf] = t[:, hf * PW:(hf + 1) * PW]

        load_half(z_sb, zv, 0, 0, "z")
        t3h = []
        mkh = []
        for hh in range(2):
            t3_t = stream.tile([P, 4 * KIN], BF16, name="t3_%d" % hh, tag="x1")
            mk_t = stream.tile([P, 4 * KIN], BF16, name="mk_%d" % hh, tag="x2")
            t3h.append(t3_t)
            mkh.append(mk_t)
        for fp in range(4):
            hh, lo = fp // 2, (fp % 2) * 2 * KIN
            nc.sync.dma_start(
                out=t3h[hh][:, lo:lo + 2 * KIN].rearrange("p (f k) -> p f k", f=2),
                in_=t3v[:, 2 * fp:2 * fp + 2, :])
            nc.sync.dma_start(
                out=mkh[hh][:, lo:lo + 2 * KIN].rearrange("p (f k) -> p f k", f=2),
                in_=mkv[:, 2 * fp:2 * fp + 2, :])
        c_sb = const.tile([P, F], BF16, name="c_sb")
        nc.scalar.dma_start(out=c_sb[:], in_=C_w)
        bias_sb = const.tile([P, O], BF16, name="bias_sb")
        nc.scalar.dma_start(out=bias_sb[:], in_=C_b.partition_broadcast(P))
        load_half(x2_sb, x2v, 0, 0, "x2")
        load_half(z_sb, zv, 0, 1, "z")
        load_half(z_sb, zv, 1, 0, "z")
        load_half(x1_sb, x1v, 0, 0, "x1")
        load_half(x2_sb, x2v, 0, 1, "x2")
        load_half(x1_sb, x1v, 0, 1, "x1")
        load_half(z_sb, zv, 1, 1, "z")
        load_half(x2_sb, x2v, 1, 0, "x2")
        load_half(x1_sb, x1v, 1, 0, "x1")
        load_whole(z_sb, zv, 2, "z")
        load_half(x2_sb, x2v, 1, 1, "x2")
        load_half(x1_sb, x1v, 1, 1, "x1")
        load_whole(z_sb, zv, 3, "z")
        later_loads = {1: (2, 4), 2: (3, 5), 3: (4, 6), 4: (5, None), 5: (None, 7), 6: (6, None), 8: (7, None)}

        zg = {}
        zc = {}
        zs = {}

        def z_t(k, g, early=False):
            if g == 0:
                zg[k] = work.tile([P, 2 * 256 * 4], BF16, name="zg_%d" % k, tag="zg", align_bytes=64)
            zw = z_sb[k].bitcast(F32)
            zt = psum.tile([P, 2, 256], F32, name="zt", tag=("p3" if early else "tp"), bufs=(5 if early else 1))
            for u in range(2):
                for jl in range(2):
                    col = jl * 512 + 256 * g + 128 * u
                    nc.tensor.transpose(zt[:, u, jl * P:(jl + 1) * P], zw[:, col:col + P], ident_f[:])
            zgw = zg[k][:].bitcast(F32).rearrange("p (g c u) -> p g c u", g=2, u=2)
            nc.scalar.copy(out=zgw[:, g, :, :], in_=zt[:].rearrange("p u c -> p c u"))

        def z_q(k):
            zc[k] = work.tile([P, 512], U32, name="zc_%d" % k, tag="zc", bufs=4, align_bytes=64)
            zs[k] = work.tile([P, 512], U8, name="zs_%d" % k, tag="zs", bufs=4, align_bytes=64)
            nc.vector.quantize_mx(out=zc[k][:].bitcast(FP8X4), scales=zs[k][:], in_=zg[k][:])

        wg = const.tile([P, 8 * 256 * 4], BF16, name="wg", align_bytes=64)
        wc = const.tile([P, 8 * 256], U32, name="wc", align_bytes=64)
        ws = const.tile([P, 8 * 256], U8, name="ws", align_bytes=64)
        wgw = wg[:].bitcast(F32).rearrange("p (g pr s r u) -> p g s pr r u", g=2, pr=4, s=16, r=16, u=2)

        def w_mul(fp, parts):
            hh, lo = fp // 2, (fp % 2) * 2 * KIN
            tv = t3h[hh][:, lo:lo + 2 * KIN].rearrange("p (f k) -> p f k", f=2)
            mv = mkh[hh][:, lo:lo + 2 * KIN].rearrange("p (f k) -> p f k", f=2)
            w = KIN // parts
            for i in range(parts):
                nc.vector.tensor_tensor(
                    out=tv[:, :, i * w:(i + 1) * w], in0=tv[:, :, i * w:(i + 1) * w],
                    in1=mv[:, :, i * w:(i + 1) * w], op=ALU.mult)

        def w_t(fp, second_on_vector):
            hh, lo = fp // 2, (fp % 2) * 2 * KIN
            ww = t3h[hh][:].bitcast(F32)
            for g in range(2):
                wt = psum.tile([P, 2, 256], F32, name="wt", tag="p3", bufs=5)
                for u in range(2):
                    for fl in range(2):
                        col = lo // 2 + fl * 512 + 256 * g + 128 * u
                        nc.tensor.transpose(wt[:, u, fl * P:(fl + 1) * P], ww[:, col:col + P], ident_f[:])
                src = wt[:].rearrange("p u (s pr r) -> p s pr r u", s=4, pr=4, r=16)
                dst = wgw[:, g, 4 * fp:4 * fp + 4, :, :, :]
                if g == 1 and second_on_vector:
                    nc.vector.tensor_copy(out=dst, in_=src)
                else:
                    nc.scalar.copy(out=dst, in_=src)

        def w_q(fp):
            for pr in range(4):
                for g in G_OF_PR[pr]:
                    lo_w = CI[(pr, g)] * 256 + 64 * fp
                    nc.vector.quantize_mx(
                        out=wc[:, lo_w:lo_w + 64].bitcast(FP8X4), scales=ws[:, lo_w:lo_w + 64],
                        in_=wg[:, 4 * lo_w:4 * lo_w + 256])

        cg = const.tile([P, 2 * O * 4], BF16, name="cg", align_bytes=64)
        cc = const.tile([P, 2 * O], U32, name="cc", align_bytes=64)
        cs = const.tile([P, 2 * O], U8, name="cs", align_bytes=64)

        def c_t():
            ct = psum.tile([P, 8, P], BF16, name="ct", tag="xt", bufs=1)
            for gt in range(8):
                nc.tensor.transpose(ct[:, gt, :], c_sb[:, gt * P:(gt + 1) * P], ident_b[:])
            nc.scalar.copy(
                out=cg[:].rearrange("p (g o t) -> p g o t", g=2, t=4),
                in_=ct[:].rearrange("p (g t) o -> p g o t", g=2))

        def c_q():
            nc.vector.quantize_mx(out=cc[:].bitcast(FP8X4), scales=cs[:], in_=cg[:])

        p3 = {}
        y_sb = {}
        x3_sb = {}
        xg = {}
        xc = {}
        xs = {}
        po = {}

        def mm1(k, pr):
            bank = psum.tile([P, 512], F32, name="p3_%d_%d" % (k, pr), tag="p3", bufs=5)
            p3[(k, pr)] = bank
            gs = G_OF_PR[pr]
            for jl in range(2):
                for g in gs:
                    lo = g * 256 + jl * P
                    ci = CI[(pr, g)]
                    nc.tensor.matmul_mx(
                        out=bank[:, jl * 256:(jl + 1) * 256],
                        lhsT=zc[k][:, lo:lo + P].bitcast(FP8X4), lhsT_scale=zs[k][:, lo:lo + P],
                        rhs=wc[:, ci * 256:(ci + 1) * 256].bitcast(FP8X4), rhs_scale=ws[:, ci * 256:(ci + 1) * 256],
                        start=(g == gs[0]), stop=(g == gs[-1]))

        def op1(k):
            y_sb[k] = work.tile([P, PW], F32, name="y_%d" % k, tag="y")
            yv = y_sb[k][:].rearrange("p (s q) -> p s q", q=64)
            x2u = x2_sb[k].rearrange("p (s q) -> p s q", q=64)
            for pr in range(4):
                nc.vector.scalar_tensor_tensor(
                    out=yv[:, :, pr * 16:(pr + 1) * 16],
                    in0=p3[(k, pr)][:].rearrange("p (s r) -> p s r", r=16),
                    scalar=2.0,
                    in1=x2u[:, :, pr * 16:(pr + 1) * 16],
                    op0=ALU.mult, op1=ALU.mult)

        def op2(k, lo, hi, eng):
            if k not in x3_sb:
                x3_sb[k] = work.tile([P, PW], BF16, name="x3_%d" % k, tag="x3", bufs=4)
            cols = slice(lo, hi)
            eng.tensor_tensor(out=x3_sb[k][:, cols], in0=y_sb[k][:, cols], in1=x1_sb[k][:, cols], op=ALU.subtract)

        def x_t(k, unit, tail=False, split=False):
            if unit == 0:
                xg[k] = work.tile([P, 2 * 1024], BF16, name="xg_%d" % k, tag="xg", bufs=4, align_bytes=64)
            dst = xg[k][:, unit * 1024:(unit + 1) * 1024].rearrange("p (g b t) -> p g b t", g=2, t=4)
            if split:
                for g in range(2):
                    xh = psum.tile([P, 4, P], BF16, name="xh", tag="p3", bufs=5)
                    for t in range(4):
                        col = unit * F + (4 * g + t) * P
                        nc.tensor.transpose(xh[:, t, :], x3_sb[k][:, col:col + P], ident_b[:])
                    if g == 0:
                        nc.scalar.copy(out=dst[:, g], in_=xh[:].rearrange("p t b -> p b t"))
                    else:
                        nc.vector.tensor_copy(out=dst[:, g], in_=xh[:].rearrange("p t b -> p b t"))
            else:
                xt = psum.tile([P, 8, P], BF16, name="xt", tag=("p3" if tail else "xt"), bufs=(5 if tail else 1))
                for gt in range(8):
                    col = unit * F + gt * P
                    if gt < N_PLAIN:
                        nc.tensor.matmul(
                            out=xt[:, gt, :], lhsT=x3_sb[k][:, col:col + P], rhs=ident_b[:], start=True, stop=True)
                    else:
                        nc.tensor.transpose(xt[:, gt, :], x3_sb[k][:, col:col + P], ident_b[:])
                nc.scalar.copy(out=dst, in_=xt[:].rearrange("p (g t) b -> p g b t", g=2))

        def x_q(k, units):
            if k not in xc:
                xc[k] = work.tile([P, 512], U32, name="xc_%d" % k, tag="xc", align_bytes=64)
                xs[k] = work.tile([P, 512], U8, name="xs_%d" % k, tag="xs", align_bytes=64)
            lo, n = units[0] * 256, len(units) * 256
            nc.vector.quantize_mx(
                out=xc[k][:, lo:lo + n].bitcast(FP8X4), scales=xs[k][:, lo:lo + n], in_=xg[k][:, 4 * lo:4 * (lo + n)])

        def mm2(k, units):
            c = k // 2
            if c not in po:
                po[c] = psum.tile([P, 4, O], F32, name="po_%d" % c, tag="po", bufs=1)
            for unit in units:
                for g in range(2):
                    lo = (unit * 2 + g) * P
                    nc.tensor.matmul_mx(
                        out=po[c][:, (k % 2) * 2 + unit, :],
                        lhsT=xc[k][:, lo:lo + P].bitcast(FP8X4), lhsT_scale=xs[k][:, lo:lo + P],
                        rhs=cc[:, g * O:(g + 1) * O].bitcast(FP8X4), rhs_scale=cs[:, g * O:(g + 1) * O],
                        start=(g == 0), stop=(g == 1))

        def fin(c):
            o_sb = work.tile([P, 4, O], F32, name="o_sb", tag="o_sb", bufs=2)
            nc.vector.tensor_tensor(
                out=o_sb[:], in0=po[c][:], in1=bias_sb[:].unsqueeze(1).to_broadcast([P, 4, O]), op=ALU.add)
            nc.sync.dma_start(out=outv[c], in_=o_sb[:].rearrange("p j o -> p (j o)"))

        mark = const.tile([P, 1], BF16, name="mark")
        BOTH = [0, 1]

        def gp_cols(k):
            return GP_LONG if ((k + 1) % 2 == 0 and k + 1 >= 6) else GP_SHORT
        z_t(0, 0, True)
        z_t(0, 1, True)
        z_q(0)
        c_t()
        c_q()
        w_mul(0, 1)
        w_t(0, False)
        w_mul(1, 1)
        w_t(1, False)
        w_mul(2, 1)
        w_q(0)
        w_t(2, False)
        w_q(1)
        w_mul(3, 2)
        w_q(2)
        w_t(3, True)
        w_q(3)
        z_t(1, 0)
        z_t(1, 1, True)
        for pr in range(4):
            mm1(0, pr)
        z_t(2, 0)
        z_t(2, 1)

        for k in range(NPAIR):
            last = k == NPAIR - 1
            if k >= 1:
                nc.gpsimd.tensor_copy(out=mark[:], in_=x3_sb[k - 1][:, F:F + 1])
                op2(k - 1, 0, gp_cols(k - 1), nc.gpsimd)
            if k in later_loads:
                cx, cz = later_loads[k]
                if cx is not None:
                    load_whole(x2_sb, x2v, cx, "x2")
                    load_whole(x1_sb, x1v, cx, "x1")
                if cz is not None:
                    load_whole(z_sb, zv, cz, "z")
            if k >= 6 and k % 2 == 0:
                fin((k - 6) // 2)
            if k == 0:
                op1(0)
                z_q(1)
            if not last:
                mm1(k + 1, 0)
                mm1(k + 1, 1)
            if k >= 2:
                x_t(k - 2, 0)
            if k + 3 < NPAIR:
                z_t(k + 3, 0)
            if not last:
                mm1(k + 1, 2)
                mm1(k + 1, 3)
            if k >= 4:
                mm2(k - 4, BOTH)
            if k >= 2:
                x_t(k - 2, 1)
            if k + 3 < NPAIR:
                z_t(k + 3, 1)
            if k >= 1:
                op1(k)
            if last:
                op2(k, 0, F, nc.vector)
                op2(k, F, PW, nc.vector)
            else:
                if k >= 3:
                    x_q(k - 3, BOTH)
                if k + 2 < NPAIR:
                    z_q(k + 2)
                op2(k, gp_cols(k), PW, nc.vector)

        x_t(NPAIR - 2, 0, True)
        x_t(NPAIR - 2, 1, True)
        x_t(NPAIR - 1, 0, True)
        x_t(NPAIR - 1, 1, True, True)
        x_q(NPAIR - 4, BOTH)
        fin(NCH - 3)
        mm2(NPAIR - 4, BOTH)
        x_q(NPAIR - 3, BOTH)
        mm2(NPAIR - 3, BOTH)
        x_q(NPAIR - 2, BOTH)
        fin(NCH - 2)
        mm2(NPAIR - 2, BOTH)
        x_q(NPAIR - 1, [0])
        mm2(NPAIR - 1, [0])
        x_q(NPAIR - 1, [1])
        mm2(NPAIR - 1, [1])
        fin(NCH - 1)
